import numpy as np
import ml_dtypes


def mxq(x, axis, fmt="e4m3"):
    dtype, down = {"e4m3": (ml_dtypes.float8_e4m3fn, 7), "e5m2": (ml_dtypes.float8_e5m2, 14)}[fmt]
    v = np.moveaxis(np.asarray(x, np.float32).astype(ml_dtypes.bfloat16).astype(np.float64), axis, -1)
    blocks = v.reshape(v.shape[:-1] + (-1, 32))
    amax = np.abs(blocks).max(-1, keepdims=True)
    byte = np.maximum(np.where(amax > 0, np.frexp(amax)[1] - 1 + 127, 0) - down, 1)
    scale = np.exp2(byte - 127.0)
    codes = (blocks / scale).astype(np.float32).astype(dtype).astype(np.float64)
    return np.moveaxis((codes * scale).reshape(v.shape), -1, axis)


WIDE = False


def mx_kscale(k):
    if not WIDE:
        return np.ones(k)
    levels = np.array([10, -10, 5, -5, 0])
    a = np.random.permutation(np.resize(levels, k // 512 * 4)).reshape(k // 512, 4)
    idx = np.arange(k)
    return np.exp2(a[idx // 512, idx % 128 // 32])


BF16 = ml_dtypes.bfloat16


def bf(x):
    return np.asarray(x, np.float32).astype(BF16)


def f64(x):
    return np.asarray(x).astype(np.float64)


B, C, H, W = 16, 256, 16, 32
K = H * W
OFFSETS = [(-1, -1), (-1, 0), (-1, 1), (0, -1), (0, 0)]
EPS = 1e-12


def setup_inputs():
    s = mx_kscale(K)
    t = 2.0 ** np.round(np.log2(s.max() / s.min()) / 2)
    r = np.where(np.arange(H) % 2 == 0, 1.0 / t, t)
    return {"x": bf(np.random.standard_normal((B, C, H, W)) * r[None, None, :, None])}


def reference(x):
    x = f64(x)
    xp = np.pad(x, ((0, 0), (0, 0), (1, 1), (1, 1)), mode="edge")
    center = x.reshape(B, C, K).transpose(0, 2, 1)
    cq = mxq(center, 1, "e4m3")
    cofe = []
    for dy, dx in OFFSETS:
        if (dy, dx) == (0, 0):
            sq = cq
        else:
            side = xp[:, :, 1 + dy:1 + dy + H, 1 + dx:1 + dx + W].reshape(B, C, K).transpose(0, 2, 1)
            sq = mxq(side, 1, "e4m3")
        co = cq.transpose(0, 2, 1) @ sq
        cofe.append(co.reshape(B, C * C))
    cofe = np.stack(cofe, axis=1)
    norm = np.sqrt((cofe ** 2).sum(-1, keepdims=True))
    return cofe / np.maximum(norm, EPS)

@@ -1,0 +1,192 @@
+from contextlib import ExitStack
+
+import concourse.mybir as mybir
+from concourse.masks import make_identity
+
+F32 = mybir.dt.float32
+BF16 = mybir.dt.bfloat16
+I32 = mybir.dt.int32
+U32 = mybir.dt.uint32
+U8 = mybir.dt.uint8
+FP8X4 = mybir.dt.float8_e4m3fn_x4
+SQUARE = mybir.ActivationFunctionType.Square
+
+B, C, H, W = 16, 256, 16, 32
+K = H * W
+EPS = 1e-12
+P = 128
+HALVES = C // P
+PACK = 4
+BLOCK_P = 8
+ROW_W = W // PACK
+
+LEFT, CENTER, RIGHT, UP = 0, 1, 2, 3
+MAPS = 4
+OFFSETS = [(LEFT, True), (CENTER, True), (RIGHT, True), (LEFT, False), (CENTER, False)]
+AHEAD = 2
+
+FLOPS = 2 * B * len(OFFSETS) * C * C * K
+
+
+def tile_cofeature_fast_pa_t_kernel(tc, x, out):
+    nc = tc.nc
+    with ExitStack() as ctx:
+        const = ctx.enter_context(tc.tile_pool(name="const", bufs=1))
+        images = ctx.enter_context(tc.tile_pool(name="images", bufs=B))
+        stage = ctx.enter_context(tc.tile_pool(name="stage", bufs=2 * MAPS))
+        packed = ctx.enter_context(tc.tile_pool(name="packed", bufs=AHEAD + 1))
+        small = ctx.enter_context(tc.tile_pool(name="small", bufs=2))
+        results = ctx.enter_context(tc.tile_pool(name="results", bufs=4 * len(OFFSETS)))
+        psum_t = ctx.enter_context(tc.psum_pool(name="psum_t", bufs=2))
+        psum_g = ctx.enter_context(tc.psum_pool(name="psum_g", bufs=len(OFFSETS)))
+        psum_n = ctx.enter_context(tc.psum_pool(name="psum_n", bufs=1))
+
+        identity = const.tile([P, P], F32)
+        make_identity(nc, identity[:])
+        ones = const.tile([P, P], F32)
+        nc.vector.memset(ones[:], 1.0)
+        edges = []
+        for e in range(AHEAD + 1):
+            edge = const.tile([P, C], U32, name="edge%d" % e, align_bytes=64)
+            nc.vector.memset(edge[:].bitcast(I32), 0)
+            edges.append(edge)
+
+        image = {}
+        grouped_of = {}
+        codes_of = {}
+        scales_of = {}
+        sums_of = {}
+        inverse_norm = {}
+
+        def load(b):
+            x_sb = images.tile([P, HALVES * (K + W)], BF16)
+            left = images.tile([P, HALVES * K], BF16)
+            right = images.tile([P, HALVES * K], BF16)
+            source = x[b].rearrange("(p h) i j -> p h (i j)", h=HALVES)
+            x_view = x_sb[:].rearrange("p (h k) -> p h k", h=HALVES)
+            left_view = left[:].rearrange("p (h k) -> p h k", h=HALVES)
+            right_view = right[:].rearrange("p (h k) -> p h k", h=HALVES)
+            nc.sync.dma_start(out=x_view[:, :, 0:K], in_=source)
+            nc.sync.dma_start(out=left_view[:, :, 1:K], in_=source[:, :, 0 : K - 1])
+            nc.sync.dma_start(out=right_view[:, :, 0 : K - 1], in_=source[:, :, 1:K])
+            nc.gpsimd.memset(x_view[:, :, K : K + W], 0.0)
+            image[b] = (x_sb, left, right)
+
+        def replicate_border(b):
+            x_sb, left, right = image[b]
+            x_rows = x_sb[:].rearrange("p (h i j) -> p h i j", h=HALVES, j=W)
+            left_rows = left[:].rearrange("p (h i j) -> p h i j", h=HALVES, j=W)
+            right_rows = right[:].rearrange("p (h i j) -> p h i j", h=HALVES, j=W)
+            nc.vector.tensor_copy(out=left_rows[:, :, :, 0:1], in_=x_rows[:, :, 0:H, 0:1])
+            nc.vector.tensor_copy(out=right_rows[:, :, :, W - 1 : W], in_=x_rows[:, :, 0:H, W - 1 : W])
+
+        def transpose_map(b, m):
+            x_sb, left, right = image[b]
+            source = {LEFT: left, CENTER: x_sb, RIGHT: right, UP: x_sb}[m]
+            first = ROW_W if m == UP else 0
+            words = source[:].bitcast(F32).rearrange("p (h w u) -> p h u w", h=HALVES, u=2)
+            turned = psum_t.tile([P, HALVES, 2, P], F32)
+            for h in range(HALVES):
+                for u in range(2):
+                    nc.tensor.transpose(turned[:, h, u, :], words[:, h, u, first : first + P], identity[:])
+            grouped = stage.tile([P, C * PACK], BF16, align_bytes=64)
+            nc.scalar.copy(
+                out=grouped[:].bitcast(F32).rearrange("p (h m u) -> p h m u", h=HALVES, u=2),
+                in_=turned[:].rearrange("p h u m -> p h m u"),
+            )
+            grouped_of[(b, m)] = grouped
+
+        def quantise_maps(b):
+            codes = packed.tile([P, MAPS, C], U32, align_bytes=64)
+            scales = packed.tile([P, MAPS, C], U8, align_bytes=64)
+            for m in range(MAPS):
+                nc.vector.quantize_mx(
+                    out=codes[:, m, :].bitcast(FP8X4), scales=scales[:, m, :], in_=grouped_of[(b, m)][:]
+                )
+            edge = edges[b % len(edges)]
+            nc.vector.tensor_copy(
+                out=edge[0:BLOCK_P, :].bitcast(I32), in_=codes[0:BLOCK_P, CENTER, :].bitcast(I32)
+            )
+            codes_of[b] = codes
+            scales_of[b] = scales
+
+        def products(b):
+            codes, scales, edge = codes_of[b], scales_of[b], edges[b % len(edges)]
+            for o, (m, row_above) in enumerate(OFFSETS):
+                sums = psum_g.tile([P, HALVES, C], F32)
+                for h in range(HALVES):
+                    cols = slice(h * P, (h + 1) * P)
+                    if row_above:
+                        stationary = [(codes[:, UP, cols], scales[:, UP, cols]), (edge[:, cols], scales[:, CENTER, cols])]
+                    else:
+                        stationary = [(codes[:, CENTER, cols], scales[:, CENTER, cols])]
+                    for n, (words, plane) in enumerate(stationary):
+                        nc.tensor.matmul_mx(
+                            out=sums[:, h, :],
+                            lhsT=words.bitcast(FP8X4),
+                            lhsT_scale=plane,
+                            rhs=codes[:, m, :].bitcast(FP8X4),
+                            rhs_scale=scales[:, m, :],
+                            start=(n == 0),
+                            stop=(n == len(stationary) - 1),
+                        )
+                sums_of[(b, o)] = sums
+
+        def squares(b):
+            partial = small.tile([P, len(OFFSETS)], F32)
+            for o in range(len(OFFSETS)):
+                squared = small.tile([P, HALVES * C], F32)
+                nc.scalar.activation(
+                    out=squared[:],
+                    in_=sums_of[(b, o)][:].rearrange("p h d -> p (h d)"),
+                    func=SQUARE,
+                    accum_out=partial[:, o : o + 1],
+                )
+            return partial
+
+        def norms(b, partial):
+            total = psum_n.tile([P, len(OFFSETS)], F32)
+            nc.tensor.matmul(out=total[:], lhsT=ones[:], rhs=partial[:], start=True, stop=True)
+            norm = small.tile([P, len(OFFSETS)], F32)
+            nc.scalar.sqrt(out=norm[:], in_=total[:])
+            floored = small.tile([P, len(OFFSETS)], F32)
+            nc.vector.tensor_scalar_max(out=floored[:], in0=norm[:], scalar1=EPS)
+            inverse = small.tile([P, len(OFFSETS)], F32)
+            nc.vector.reciprocal(out=inverse[:], in_=floored[:])
+            inverse_norm[b] = inverse
+
+        def scale_and_store(b):
+            for o in range(len(OFFSETS)):
+                result = results.tile([P, HALVES * C], F32)
+                nc.vector.tensor_scalar_mul(
+                    out=result[:].rearrange("p (h m g) -> p h m g", h=HALVES, g=HALVES),
+                    in0=sums_of[(b, o)][:].rearrange("p h (g m) -> p h m g", g=HALVES),
+                    scalar1=inverse_norm[b][:, o : o + 1],
+                )
+                nc.sync.dma_start(out=out[b, o].rearrange("(p f) -> p f", p=P), in_=result[:])
+
+        for b in range(B):
+            load(b)
+        for b in range(AHEAD):
+            replicate_border(b)
+            for m in range(MAPS):
+                transpose_map(b, m)
+            quantise_maps(b)
+        replicate_border(AHEAD)
+        products(0)
+        for b in range(B):
+            ready = b + AHEAD
+            partial = squares(b)
+            if ready < B:
+                transpose_map(ready, 0)
+            norms(b, partial)
+            if ready < B:
+                for m in range(1, MAPS):
+                    transpose_map(ready, m)
+            scale_and_store(b)
+            if b + 1 < B:
+                products(b + 1)
+            if ready < B:
+                quantise_maps(ready)
+            if ready + 1 < B:
+                replicate_border(ready + 1)

@@ -10,6 +10,9 @@ U32 = mybir.dt.uint32
 U8 = mybir.dt.uint8
 FP8X4 = mybir.dt.float8_e4m3fn_x4
 SQUARE = mybir.ActivationFunctionType.Square
+COPY = mybir.ActivationFunctionType.Copy
+MULT = mybir.AluOpType.mult
+ADD = mybir.AluOpType.add
 
 B, C, H, W = 16, 256, 16, 32
 K = H * W
@@ -24,6 +27,7 @@ LEFT, CENTER, RIGHT, UP = 0, 1, 2, 3
 MAPS = 4
 OFFSETS = [(LEFT, True), (CENTER, True), (RIGHT, True), (LEFT, False), (CENTER, False)]
 AHEAD = 2
+LOADS_AHEAD = 5
 
 FLOPS = 2 * B * len(OFFSETS) * C * C * K
 
@@ -35,11 +39,12 @@ def tile_cofeature_fast_pa_t_kernel(tc, x, out):
         images = ctx.enter_context(tc.tile_pool(name="images", bufs=B))
         stage = ctx.enter_context(tc.tile_pool(name="stage", bufs=2 * MAPS))
         packed = ctx.enter_context(tc.tile_pool(name="packed", bufs=AHEAD + 1))
-        small = ctx.enter_context(tc.tile_pool(name="small", bufs=2))
+        small = ctx.enter_context(tc.tile_pool(name="small", bufs=3))
         results = ctx.enter_context(tc.tile_pool(name="results", bufs=4 * len(OFFSETS)))
-        psum_t = ctx.enter_context(tc.psum_pool(name="psum_t", bufs=2))
-        psum_g = ctx.enter_context(tc.psum_pool(name="psum_g", bufs=len(OFFSETS)))
+        psum_t = ctx.enter_context(tc.psum_pool(name="psum_t", bufs=3))
+        psum_g = ctx.enter_context(tc.psum_pool(name="psum_g", bufs=4))
         psum_n = ctx.enter_context(tc.psum_pool(name="psum_n", bufs=1))
+        ctx.enter_context(tc.manual_schedule())
 
         identity = const.tile([P, P], F32)
         make_identity(nc, identity[:])
@@ -55,8 +60,8 @@ def tile_cofeature_fast_pa_t_kernel(tc, x, out):
         grouped_of = {}
         codes_of = {}
         scales_of = {}
-        sums_of = {}
-        inverse_norm = {}
+        partial_of = {}
+        result_of = {}
 
         def load(b):
             x_sb = images.tile([P, HALVES * (K + W)], BF16)
@@ -80,7 +85,7 @@ def tile_cofeature_fast_pa_t_kernel(tc, x, out):
             nc.vector.tensor_copy(out=left_rows[:, :, :, 0:1], in_=x_rows[:, :, 0:H, 0:1])
             nc.vector.tensor_copy(out=right_rows[:, :, :, W - 1 : W], in_=x_rows[:, :, 0:H, W - 1 : W])
 
-        def transpose_map(b, m):
+        def transpose_map(b, m, on_vector):
             x_sb, left, right = image[b]
             source = {LEFT: left, CENTER: x_sb, RIGHT: right, UP: x_sb}[m]
             first = ROW_W if m == UP else 0
@@ -90,7 +95,8 @@ def tile_cofeature_fast_pa_t_kernel(tc, x, out):
                 for u in range(2):
                     nc.tensor.transpose(turned[:, h, u, :], words[:, h, u, first : first + P], identity[:])
             grouped = stage.tile([P, C * PACK], BF16, align_bytes=64)
-            nc.scalar.copy(
+            copy = nc.vector.tensor_copy if on_vector else nc.scalar.copy
+            copy(
                 out=grouped[:].bitcast(F32).rearrange("p (h m u) -> p h m u", h=HALVES, u=2),
                 in_=turned[:].rearrange("p h u m -> p h m u"),
             )
@@ -110,83 +116,92 @@ def tile_cofeature_fast_pa_t_kernel(tc, x, out):
             codes_of[b] = codes
             scales_of[b] = scales
 
-        def products(b):
+        def product(b, o):
             codes, scales, edge = codes_of[b], scales_of[b], edges[b % len(edges)]
-            for o, (m, row_above) in enumerate(OFFSETS):
-                sums = psum_g.tile([P, HALVES, C], F32)
-                for h in range(HALVES):
-                    cols = slice(h * P, (h + 1) * P)
-                    if row_above:
-                        stationary = [(codes[:, UP, cols], scales[:, UP, cols]), (edge[:, cols], scales[:, CENTER, cols])]
-                    else:
-                        stationary = [(codes[:, CENTER, cols], scales[:, CENTER, cols])]
-                    for n, (words, plane) in enumerate(stationary):
-                        nc.tensor.matmul_mx(
-                            out=sums[:, h, :],
-                            lhsT=words.bitcast(FP8X4),
-                            lhsT_scale=plane,
-                            rhs=codes[:, m, :].bitcast(FP8X4),
-                            rhs_scale=scales[:, m, :],
-                            start=(n == 0),
-                            stop=(n == len(stationary) - 1),
-                        )
-                sums_of[(b, o)] = sums
+            m, row_above = OFFSETS[o]
+            sums = psum_g.tile([P, HALVES, C], F32)
+            for h in range(HALVES):
+                cols = slice(h * P, (h + 1) * P)
+                if row_above:
+                    stationary = [(codes[:, UP, cols], scales[:, UP, cols]), (edge[:, cols], scales[:, CENTER, cols])]
+                else:
+                    stationary = [(codes[:, CENTER, cols], scales[:, CENTER, cols])]
+                for n, (words, plane) in enumerate(stationary):
+                    nc.tensor.matmul_mx(
+                        out=sums[:, h, :],
+                        lhsT=words.bitcast(FP8X4),
+                        lhsT_scale=plane,
+                        rhs=codes[:, m, :].bitcast(FP8X4),
+                        rhs_scale=scales[:, m, :],
+                        start=(n == 0),
+                        stop=(n == len(stationary) - 1),
+                    )
+            squared = small.tile([P, HALVES * C], F32)
+            nc.scalar.activation(
+                out=squared[:],
+                in_=sums[:].rearrange("p h d -> p (h d)"),
+                func=SQUARE,
+                accum_out=partial_of[b][:, o : o + 1],
+            )
+            result = results.tile([P, HALVES * C], F32)
+            nc.vector.tensor_copy(
+                out=result[:].rearrange("p (h m g) -> p h m g", h=HALVES, g=HALVES),
+                in_=sums[:].rearrange("p h (g m) -> p h m g", g=HALVES),
+            )
+            result_of[(b, o)] = result
 
-        def squares(b):
-            partial = small.tile([P, len(OFFSETS)], F32)
-            for o in range(len(OFFSETS)):
-                squared = small.tile([P, HALVES * C], F32)
-                nc.scalar.activation(
-                    out=squared[:],
-                    in_=sums_of[(b, o)][:].rearrange("p h d -> p (h d)"),
-                    func=SQUARE,
-                    accum_out=partial[:, o : o + 1],
-                )
-            return partial
-
-        def norms(b, partial):
+        def normalise_and_store(b):
             total = psum_n.tile([P, len(OFFSETS)], F32)
-            nc.tensor.matmul(out=total[:], lhsT=ones[:], rhs=partial[:], start=True, stop=True)
+            nc.tensor.matmul(out=total[:], lhsT=ones[:], rhs=partial_of[b][:], start=True, stop=True)
             norm = small.tile([P, len(OFFSETS)], F32)
             nc.scalar.sqrt(out=norm[:], in_=total[:])
             floored = small.tile([P, len(OFFSETS)], F32)
             nc.vector.tensor_scalar_max(out=floored[:], in0=norm[:], scalar1=EPS)
             inverse = small.tile([P, len(OFFSETS)], F32)
             nc.vector.reciprocal(out=inverse[:], in_=floored[:])
-            inverse_norm[b] = inverse
-
-        def scale_and_store(b):
             for o in range(len(OFFSETS)):
-                result = results.tile([P, HALVES * C], F32)
-                nc.vector.tensor_scalar_mul(
-                    out=result[:].rearrange("p (h m g) -> p h m g", h=HALVES, g=HALVES),
-                    in0=sums_of[(b, o)][:].rearrange("p h (g m) -> p h m g", g=HALVES),
-                    scalar1=inverse_norm[b][:, o : o + 1],
-                )
+                result = result_of[(b, o)]
+                factor = inverse[:, o : o + 1]
+                if b < B - 1:
+                    nc.gpsimd.tensor_scalar(
+                        out=result[:], in0=result[:], scalar1=factor, scalar2=0.0, op0=MULT, op1=ADD
+                    )
+                elif o % 2 == 0:
+                    nc.vector.tensor_scalar_mul(out=result[:], in0=result[:], scalar1=factor)
+                else:
+                    nc.scalar.activation(out=result[:], in_=result[:], func=COPY, scale=factor)
                 nc.sync.dma_start(out=out[b, o].rearrange("(p f) -> p f", p=P), in_=result[:])
 
-        for b in range(B):
+        for b in range(LOADS_AHEAD):
             load(b)
         for b in range(AHEAD):
             replicate_border(b)
             for m in range(MAPS):
-                transpose_map(b, m)
+                transpose_map(b, m, on_vector=(m % 2 == 1))
             quantise_maps(b)
         replicate_border(AHEAD)
-        products(0)
+        replicate_border(AHEAD + 1)
         for b in range(B):
             ready = b + AHEAD
-            partial = squares(b)
+            if b + LOADS_AHEAD < B:
+                load(b + LOADS_AHEAD)
+            if ready + 2 < B:
+                replicate_border(ready + 2)
+            partial = small.tile([P, len(OFFSETS)], F32)
+            partial_of[b] = partial
             if ready < B:
-                transpose_map(ready, 0)
-            norms(b, partial)
+                transpose_map(ready, LEFT, on_vector=False)
+                transpose_map(ready, CENTER, on_vector=False)
+            product(b, 0)
+            product(b, 1)
+            if b > 0:
+                normalise_and_store(b - 1)
             if ready < B:
-                for m in range(1, MAPS):
-                    transpose_map(ready, m)
-            scale_and_store(b)
-            if b + 1 < B:
-                products(b + 1)
+                transpose_map(ready, RIGHT, on_vector=False)
+                transpose_map(ready, UP, on_vector=True)
+            product(b, 2)
+            product(b, 3)
+            product(b, 4)
             if ready < B:
                 quantise_maps(ready)
-            if ready + 1 < B:
-                replicate_border(ready + 1)
+        normalise_and_store(B - 1)

@@ -26,10 +26,12 @@ ROW_W = W // PACK
 LEFT, CENTER, RIGHT, UP = 0, 1, 2, 3
 MAPS = 4
 OFFSETS = [(LEFT, True), (CENTER, True), (RIGHT, True), (LEFT, False), (CENTER, False)]
+N_OFF = len(OFFSETS)
+KEPT = 2
 AHEAD = 2
 LOADS_AHEAD = 5
 
-FLOPS = 2 * B * len(OFFSETS) * C * C * K
+FLOPS = 2 * B * N_OFF * C * C * K
 
 
 def tile_cofeature_fast_pa_t_kernel(tc, x, out):
@@ -37,10 +39,10 @@ def tile_cofeature_fast_pa_t_kernel(tc, x, out):
     with ExitStack() as ctx:
         const = ctx.enter_context(tc.tile_pool(name="const", bufs=1))
         images = ctx.enter_context(tc.tile_pool(name="images", bufs=B))
-        stage = ctx.enter_context(tc.tile_pool(name="stage", bufs=2 * MAPS))
+        stage = ctx.enter_context(tc.tile_pool(name="stage", bufs=3 * MAPS))
         packed = ctx.enter_context(tc.tile_pool(name="packed", bufs=AHEAD + 1))
         small = ctx.enter_context(tc.tile_pool(name="small", bufs=3))
-        results = ctx.enter_context(tc.tile_pool(name="results", bufs=4 * len(OFFSETS)))
+        results = ctx.enter_context(tc.tile_pool(name="results", bufs=4 * N_OFF))
         psum_t = ctx.enter_context(tc.psum_pool(name="psum_t", bufs=3))
         psum_g = ctx.enter_context(tc.psum_pool(name="psum_g", bufs=4))
         psum_n = ctx.enter_context(tc.psum_pool(name="psum_n", bufs=1))
@@ -57,10 +59,12 @@ def tile_cofeature_fast_pa_t_kernel(tc, x, out):
             edges.append(edge)
 
         image = {}
+        turned_of = {}
         grouped_of = {}
         codes_of = {}
         scales_of = {}
         partial_of = {}
+        sums_of = {}
         result_of = {}
 
         def load(b):
@@ -82,10 +86,10 @@ def tile_cofeature_fast_pa_t_kernel(tc, x, out):
             x_rows = x_sb[:].rearrange("p (h i j) -> p h i j", h=HALVES, j=W)
             left_rows = left[:].rearrange("p (h i j) -> p h i j", h=HALVES, j=W)
             right_rows = right[:].rearrange("p (h i j) -> p h i j", h=HALVES, j=W)
-            nc.vector.tensor_copy(out=left_rows[:, :, :, 0:1], in_=x_rows[:, :, 0:H, 0:1])
-            nc.vector.tensor_copy(out=right_rows[:, :, :, W - 1 : W], in_=x_rows[:, :, 0:H, W - 1 : W])
+            nc.gpsimd.tensor_copy(out=left_rows[:, :, :, 0:1], in_=x_rows[:, :, 0:H, 0:1])
+            nc.gpsimd.tensor_copy(out=right_rows[:, :, :, W - 1 : W], in_=x_rows[:, :, 0:H, W - 1 : W])
 
-        def transpose_map(b, m, on_vector):
+        def transpose_map(b, m):
             x_sb, left, right = image[b]
             source = {LEFT: left, CENTER: x_sb, RIGHT: right, UP: x_sb}[m]
             first = ROW_W if m == UP else 0
@@ -94,11 +98,14 @@ def tile_cofeature_fast_pa_t_kernel(tc, x, out):
             for h in range(HALVES):
                 for u in range(2):
                     nc.tensor.transpose(turned[:, h, u, :], words[:, h, u, first : first + P], identity[:])
+            turned_of[(b, m)] = turned
+
+        def copy_out(b, m, on_vector):
             grouped = stage.tile([P, C * PACK], BF16, align_bytes=64)
             copy = nc.vector.tensor_copy if on_vector else nc.scalar.copy
             copy(
                 out=grouped[:].bitcast(F32).rearrange("p (h m u) -> p h m u", h=HALVES, u=2),
-                in_=turned[:].rearrange("p h u m -> p h m u"),
+                in_=turned_of[(b, m)][:].rearrange("p h u m -> p h m u"),
             )
             grouped_of[(b, m)] = grouped
 
@@ -115,6 +122,9 @@ def tile_cofeature_fast_pa_t_kernel(tc, x, out):
             )
             codes_of[b] = codes
             scales_of[b] = scales
+
+        def in_output_order(sums):
+            return sums[:].rearrange("p h (g m) -> p h m g", g=HALVES)
 
         def product(b, o):
             codes, scales, edge = codes_of[b], scales_of[b], edges[b % len(edges)]
@@ -143,65 +153,81 @@ def tile_cofeature_fast_pa_t_kernel(tc, x, out):
                 func=SQUARE,
                 accum_out=partial_of[b][:, o : o + 1],
             )
-            result = results.tile([P, HALVES * C], F32)
-            nc.vector.tensor_copy(
-                out=result[:].rearrange("p (h m g) -> p h m g", h=HALVES, g=HALVES),
-                in_=sums[:].rearrange("p h (g m) -> p h m g", g=HALVES),
-            )
-            result_of[(b, o)] = result
+            sums_of[(b, o)] = sums
+            if o < N_OFF - KEPT:
+                result = results.tile([P, HALVES * C], F32)
+                nc.vector.tensor_copy(
+                    out=result[:].rearrange("p (h m g) -> p h m g", h=HALVES, g=HALVES), in_=in_output_order(sums)
+                )
+                result_of[(b, o)] = result
+
+        def store(b, o, result):
+            nc.sync.dma_start(out=out[b, o].rearrange("(p f) -> p f", p=P), in_=result[:])
 
         def normalise_and_store(b):
-            total = psum_n.tile([P, len(OFFSETS)], F32)
+            total = psum_n.tile([P, N_OFF], F32)
             nc.tensor.matmul(out=total[:], lhsT=ones[:], rhs=partial_of[b][:], start=True, stop=True)
-            norm = small.tile([P, len(OFFSETS)], F32)
+            norm = small.tile([P, N_OFF], F32)
             nc.scalar.sqrt(out=norm[:], in_=total[:])
-            floored = small.tile([P, len(OFFSETS)], F32)
+            floored = small.tile([P, N_OFF], F32)
             nc.vector.tensor_scalar_max(out=floored[:], in0=norm[:], scalar1=EPS)
-            inverse = small.tile([P, len(OFFSETS)], F32)
+            inverse = small.tile([P, N_OFF], F32)
             nc.vector.reciprocal(out=inverse[:], in_=floored[:])
-            for o in range(len(OFFSETS)):
+            for o in range(N_OFF - KEPT, N_OFF):
+                result = results.tile([P, HALVES * C], F32)
+                nc.vector.tensor_scalar_mul(
+                    out=result[:].rearrange("p (h m g) -> p h m g", h=HALVES, g=HALVES),
+                    in0=in_output_order(sums_of[(b, o)]),
+                    scalar1=inverse[:, o : o + 1],
+                )
+                store(b, o, result)
+            for o in range(N_OFF - KEPT):
                 result = result_of[(b, o)]
                 factor = inverse[:, o : o + 1]
-                if b < B - 1:
+                if b == B - 1 and o % 2 == 0:
+                    nc.scalar.activation(out=result[:], in_=result[:], func=COPY, scale=factor)
+                else:
                     nc.gpsimd.tensor_scalar(
                         out=result[:], in0=result[:], scalar1=factor, scalar2=0.0, op0=MULT, op1=ADD
                     )
-                elif o % 2 == 0:
-                    nc.vector.tensor_scalar_mul(out=result[:], in0=result[:], scalar1=factor)
-                else:
-                    nc.scalar.activation(out=result[:], in_=result[:], func=COPY, scale=factor)
-                nc.sync.dma_start(out=out[b, o].rearrange("(p f) -> p f", p=P), in_=result[:])
+                store(b, o, result)
 
         for b in range(LOADS_AHEAD):
             load(b)
         for b in range(AHEAD):
             replicate_border(b)
             for m in range(MAPS):
-                transpose_map(b, m, on_vector=(m % 2 == 1))
-            quantise_maps(b)
+                transpose_map(b, m)
+                copy_out(b, m, on_vector=(m % 2 == 1))
+            if b < AHEAD - 1:
+                quantise_maps(b)
         replicate_border(AHEAD)
         replicate_border(AHEAD + 1)
         for b in range(B):
-            ready = b + AHEAD
+            turning = b + AHEAD
             if b + LOADS_AHEAD < B:
                 load(b + LOADS_AHEAD)
-            if ready + 2 < B:
-                replicate_border(ready + 2)
-            partial = small.tile([P, len(OFFSETS)], F32)
-            partial_of[b] = partial
-            if ready < B:
-                transpose_map(ready, LEFT, on_vector=False)
-                transpose_map(ready, CENTER, on_vector=False)
-            product(b, 0)
-            product(b, 1)
+            if turning < B:
+                transpose_map(turning, LEFT)
+                transpose_map(turning, CENTER)
+                transpose_map(turning, RIGHT)
+                copy_out(turning, LEFT, on_vector=False)
+                copy_out(turning, CENTER, on_vector=False)
+            if turning - 1 < B:
+                quantise_maps(turning - 1)
             if b > 0:
                 normalise_and_store(b - 1)
-            if ready < B:
-                transpose_map(ready, RIGHT, on_vector=False)
-                transpose_map(ready, UP, on_vector=True)
+            if turning + 2 < B:
+                replicate_border(turning + 2)
+            partial = small.tile([P, N_OFF], F32)
+            partial_of[b] = partial
+            product(b, 0)
+            product(b, 1)
+            if turning < B:
+                copy_out(turning, RIGHT, on_vector=False)
+                transpose_map(turning, UP)
+                copy_out(turning, UP, on_vector=True)
             product(b, 2)
             product(b, 3)
             product(b, 4)
-            if ready < B:
-                quantise_maps(ready)
         normalise_and_store(B - 1)

@@ -27,7 +27,7 @@ LEFT, CENTER, RIGHT, UP = 0, 1, 2, 3
 MAPS = 4
 OFFSETS = [(LEFT, True), (CENTER, True), (RIGHT, True), (LEFT, False), (CENTER, False)]
 N_OFF = len(OFFSETS)
-KEPT = 2
+KEPT = 1
 AHEAD = 2
 LOADS_AHEAD = 5
 
@@ -196,9 +196,9 @@ def tile_cofeature_fast_pa_t_kernel(tc, x, out):
             load(b)
         for b in range(AHEAD):
             replicate_border(b)
-            for m in range(MAPS):
+            for n, m in enumerate([CENTER, UP, LEFT, RIGHT]):
                 transpose_map(b, m)
-                copy_out(b, m, on_vector=(m % 2 == 1))
+                copy_out(b, m, on_vector=(n % 2 == 1))
             if b < AHEAD - 1:
                 quantise_maps(b)
         replicate_border(AHEAD)

@@ -52,6 +52,8 @@ def tile_cofeature_fast_pa_t_kernel(tc, x, out):
         make_identity(nc, identity[:])
         ones = const.tile([P, P], F32)
         nc.vector.memset(ones[:], 1.0)
+        warm = const.tile([P, 1], F32)
+        nc.scalar.sqrt(out=warm[:], in_=ones[:, 0:1])
         edges = []
         for e in range(AHEAD + 1):
             edge = const.tile([P, C], U32, name="edge%d" % e, align_bytes=64)
@@ -71,13 +73,11 @@ def tile_cofeature_fast_pa_t_kernel(tc, x, out):
             x_sb = images.tile([P, HALVES * (K + W)], BF16)
             left = images.tile([P, HALVES * K], BF16)
             right = images.tile([P, HALVES * K], BF16)
-            source = x[b].rearrange("(p h) i j -> p h (i j)", h=HALVES)
             x_view = x_sb[:].rearrange("p (h k) -> p h k", h=HALVES)
-            left_view = left[:].rearrange("p (h k) -> p h k", h=HALVES)
-            right_view = right[:].rearrange("p (h k) -> p h k", h=HALVES)
-            nc.sync.dma_start(out=x_view[:, :, 0:K], in_=source)
-            nc.sync.dma_start(out=left_view[:, :, 1:K], in_=source[:, :, 0 : K - 1])
-            nc.sync.dma_start(out=right_view[:, :, 0 : K - 1], in_=source[:, :, 1:K])
+            nc.sync.dma_start(out=x_view[:, :, 0:K], in_=x[b].rearrange("(p h) i j -> p h (i j)", h=HALVES))
+            pair = x[b].rearrange("(p h) i j -> p (h i j)", h=HALVES)
+            nc.sync.dma_start(out=left[:, 1 : HALVES * K], in_=pair[:, 0 : HALVES * K - 1])
+            nc.sync.dma_start(out=right[:, 0 : HALVES * K - 1], in_=pair[:, 1 : HALVES * K])
             nc.gpsimd.memset(x_view[:, :, K : K + W], 0.0)
             image[b] = (x_sb, left, right)
 
@@ -117,7 +117,7 @@ def tile_cofeature_fast_pa_t_kernel(tc, x, out):
                     out=codes[:, m, :].bitcast(FP8X4), scales=scales[:, m, :], in_=grouped_of[(b, m)][:]
                 )
             edge = edges[b % len(edges)]
-            nc.vector.tensor_copy(
+            nc.sync.dma_start(
                 out=edge[0:BLOCK_P, :].bitcast(I32), in_=codes[0:BLOCK_P, CENTER, :].bitcast(I32)
             )
             codes_of[b] = codes
@@ -164,16 +164,17 @@ def tile_cofeature_fast_pa_t_kernel(tc, x, out):
         def store(b, o, result):
             nc.sync.dma_start(out=out[b, o].rearrange("(p f) -> p f", p=P), in_=result[:])
 
-        def normalise_and_store(b):
+        def normalise_and_store(b, first, end):
+            these = slice(first, end)
             total = psum_n.tile([P, N_OFF], F32)
-            nc.tensor.matmul(out=total[:], lhsT=ones[:], rhs=partial_of[b][:], start=True, stop=True)
+            nc.tensor.matmul(out=total[:, these], lhsT=ones[:], rhs=partial_of[b][:, these], start=True, stop=True)
             norm = small.tile([P, N_OFF], F32)
-            nc.scalar.sqrt(out=norm[:], in_=total[:])
+            nc.scalar.sqrt(out=norm[:, these], in_=total[:, these])
             floored = small.tile([P, N_OFF], F32)
-            nc.vector.tensor_scalar_max(out=floored[:], in0=norm[:], scalar1=EPS)
+            nc.vector.tensor_scalar_max(out=floored[:, these], in0=norm[:, these], scalar1=EPS)
             inverse = small.tile([P, N_OFF], F32)
-            nc.vector.reciprocal(out=inverse[:], in_=floored[:])
-            for o in range(N_OFF - KEPT, N_OFF):
+            nc.vector.reciprocal(out=inverse[:, these], in_=floored[:, these])
+            for o in range(max(first, N_OFF - KEPT), end):
                 result = results.tile([P, HALVES * C], F32)
                 nc.vector.tensor_scalar_mul(
                     out=result[:].rearrange("p (h m g) -> p h m g", h=HALVES, g=HALVES),
@@ -181,10 +182,10 @@ def tile_cofeature_fast_pa_t_kernel(tc, x, out):
                     scalar1=inverse[:, o : o + 1],
                 )
                 store(b, o, result)
-            for o in range(N_OFF - KEPT):
+            for o in range(first, min(end, N_OFF - KEPT)):
                 result = result_of[(b, o)]
                 factor = inverse[:, o : o + 1]
-                if b == B - 1 and o % 2 == 0:
+                if b == B - 1 and end == N_OFF:
                     nc.scalar.activation(out=result[:], in_=result[:], func=COPY, scale=factor)
                 else:
                     nc.gpsimd.tensor_scalar(
@@ -205,8 +206,6 @@ def tile_cofeature_fast_pa_t_kernel(tc, x, out):
         replicate_border(AHEAD + 1)
         for b in range(B):
             turning = b + AHEAD
-            if b + LOADS_AHEAD < B:
-                load(b + LOADS_AHEAD)
             if turning < B:
                 transpose_map(turning, LEFT)
                 transpose_map(turning, CENTER)
@@ -215,8 +214,10 @@ def tile_cofeature_fast_pa_t_kernel(tc, x, out):
                 copy_out(turning, CENTER, on_vector=False)
             if turning - 1 < B:
                 quantise_maps(turning - 1)
+            if b + LOADS_AHEAD < B:
+                load(b + LOADS_AHEAD)
             if b > 0:
-                normalise_and_store(b - 1)
+                normalise_and_store(b - 1, 0, N_OFF)
             if turning + 2 < B:
                 replicate_border(turning + 2)
             partial = small.tile([P, N_OFF], F32)
@@ -228,6 +229,8 @@ def tile_cofeature_fast_pa_t_kernel(tc, x, out):
                 transpose_map(turning, UP)
                 copy_out(turning, UP, on_vector=True)
             product(b, 2)
+            if b == B - 1:
+                normalise_and_store(b, 0, 3)
             product(b, 3)
             product(b, 4)
-        normalise_and_store(B - 1)
+        normalise_and_store(B - 1, 3, N_OFF)

@@ -21,15 +21,16 @@ P = 128
 HALVES = C // P
 PACK = 4
 BLOCK_P = 8
-ROW_W = W // PACK
+SHIFTED_P = P - BLOCK_P
 
 LEFT, CENTER, RIGHT, UP = 0, 1, 2, 3
 MAPS = 4
 OFFSETS = [(LEFT, True), (CENTER, True), (RIGHT, True), (LEFT, False), (CENTER, False)]
 N_OFF = len(OFFSETS)
+ORDER = [3, 4, 0, 1, 2]
 KEPT = 1
 AHEAD = 2
-LOADS_AHEAD = 5
+LOADS_AHEAD = 6
 
 FLOPS = 2 * B * N_OFF * C * C * K
 
@@ -39,12 +40,13 @@ def tile_cofeature_fast_pa_t_kernel(tc, x, out):
     with ExitStack() as ctx:
         const = ctx.enter_context(tc.tile_pool(name="const", bufs=1))
         images = ctx.enter_context(tc.tile_pool(name="images", bufs=B))
-        stage = ctx.enter_context(tc.tile_pool(name="stage", bufs=3 * MAPS))
-        packed = ctx.enter_context(tc.tile_pool(name="packed", bufs=AHEAD + 1))
+        stage = ctx.enter_context(tc.tile_pool(name="stage", bufs=3 * (MAPS - 1)))
+        packed = ctx.enter_context(tc.tile_pool(name="packed", bufs=3))
+        planes = ctx.enter_context(tc.tile_pool(name="planes", bufs=AHEAD + 2))
         small = ctx.enter_context(tc.tile_pool(name="small", bufs=3))
         results = ctx.enter_context(tc.tile_pool(name="results", bufs=4 * N_OFF))
-        psum_t = ctx.enter_context(tc.psum_pool(name="psum_t", bufs=3))
-        psum_g = ctx.enter_context(tc.psum_pool(name="psum_g", bufs=4))
+        psum_t = ctx.enter_context(tc.psum_pool(name="psum_t", bufs=2))
+        psum_g = ctx.enter_context(tc.psum_pool(name="psum_g", bufs=5))
         psum_n = ctx.enter_context(tc.psum_pool(name="psum_n", bufs=1))
         ctx.enter_context(tc.manual_schedule())
 
@@ -55,49 +57,69 @@ def tile_cofeature_fast_pa_t_kernel(tc, x, out):
         warm = const.tile([P, 1], F32)
         nc.scalar.sqrt(out=warm[:], in_=ones[:, 0:1])
         edges = []
+        raised = []
         for e in range(AHEAD + 1):
             edge = const.tile([P, C], U32, name="edge%d" % e, align_bytes=64)
             nc.vector.memset(edge[:].bitcast(I32), 0)
             edges.append(edge)
+            up = const.tile([P, C * PACK], BF16, name="up%d" % e, align_bytes=64)
+            nc.vector.memset(up[:].bitcast(I32), 0)
+            raised.append(up)
 
         image = {}
+        ends_of = {}
         turned_of = {}
         grouped_of = {}
         codes_of = {}
         scales_of = {}
         partial_of = {}
         sums_of = {}
+        floored_of = {}
+        norm_of = {}
         result_of = {}
 
         def load(b):
-            x_sb = images.tile([P, HALVES * (K + W)], BF16)
+            x_sb = images.tile([P, HALVES * K], BF16)
             left = images.tile([P, HALVES * K], BF16)
-            right = images.tile([P, HALVES * K], BF16)
-            x_view = x_sb[:].rearrange("p (h k) -> p h k", h=HALVES)
-            nc.sync.dma_start(out=x_view[:, :, 0:K], in_=x[b].rearrange("(p h) i j -> p h (i j)", h=HALVES))
             pair = x[b].rearrange("(p h) i j -> p (h i j)", h=HALVES)
+            nc.sync.dma_start(out=x_sb[:], in_=pair)
             nc.sync.dma_start(out=left[:, 1 : HALVES * K], in_=pair[:, 0 : HALVES * K - 1])
-            nc.sync.dma_start(out=right[:, 0 : HALVES * K - 1], in_=pair[:, 1 : HALVES * K])
-            nc.gpsimd.memset(x_view[:, :, K : K + W], 0.0)
-            image[b] = (x_sb, left, right)
+            image[b] = (x_sb, left)
 
-        def replicate_border(b):
-            x_sb, left, right = image[b]
-            x_rows = x_sb[:].rearrange("p (h i j) -> p h i j", h=HALVES, j=W)
-            left_rows = left[:].rearrange("p (h i j) -> p h i j", h=HALVES, j=W)
-            right_rows = right[:].rearrange("p (h i j) -> p h i j", h=HALVES, j=W)
-            nc.gpsimd.tensor_copy(out=left_rows[:, :, :, 0:1], in_=x_rows[:, :, 0:H, 0:1])
-            nc.gpsimd.tensor_copy(out=right_rows[:, :, :, W - 1 : W], in_=x_rows[:, :, 0:H, W - 1 : W])
+        def copy_on_gpsimd(dst, src):
+            nc.gpsimd.tensor_scalar(out=dst, in0=src, scalar1=1.0, scalar2=0.0, op0=MULT, op1=ADD)
+
+        def copy_on_vector(dst, src):
+            nc.vector.tensor_copy(out=dst, in_=src)
+
+        def replicate_border(b, copy):
+            x_sb, left = image[b]
+            rows = x_sb[:].rearrange("p (r j) -> p r j", j=W)
+            copy(left[:].rearrange("p (r j) -> p r j", j=W)[:, :, 0:1], rows[:, :, 0:1])
+            ends = planes.tile([P, HALVES, P, 2], BF16)
+            by_row = ends[:].rearrange("p h (i q) e -> p (h i) q e", q=BLOCK_P)
+            copy(
+                by_row[:, :, 0 : BLOCK_P - 1, :],
+                rows[:, :, PACK - 1 : W - 1].rearrange("p r (q t) -> p r q t", t=PACK)[:, :, :, 0:2],
+            )
+            copy(by_row[:, :, BLOCK_P - 1, :], rows[:, :, W - 1 : W].to_broadcast([P, HALVES * H, 2]))
+            ends_of[b] = ends
 
         def transpose_map(b, m):
-            x_sb, left, right = image[b]
-            source = {LEFT: left, CENTER: x_sb, RIGHT: right, UP: x_sb}[m]
-            first = ROW_W if m == UP else 0
-            words = source[:].bitcast(F32).rearrange("p (h w u) -> p h u w", h=HALVES, u=2)
+            x_sb, left = image[b]
+            words_of = [
+                source[:].bitcast(F32).rearrange("p (h w u) -> p h u w", h=HALVES, u=2) for source in (x_sb, left)
+            ]
             turned = psum_t.tile([P, HALVES, 2, P], F32)
             for h in range(HALVES):
+                ends = ends_of[b][:, h].rearrange("p m e -> p (m e)").bitcast(F32)
+                words = {
+                    CENTER: [words_of[0][:, h, 0, :], words_of[0][:, h, 1, :]],
+                    LEFT: [words_of[1][:, h, 0, :], words_of[1][:, h, 1, :]],
+                    RIGHT: [words_of[1][:, h, 1, :], ends],
+                }[m]
                 for u in range(2):
-                    nc.tensor.transpose(turned[:, h, u, :], words[:, h, u, first : first + P], identity[:])
+                    nc.tensor.transpose(turned[:, h, u, :], words[u], identity[:])
             turned_of[(b, m)] = turned
 
         def copy_out(b, m, on_vector):
@@ -109,19 +131,27 @@ def tile_cofeature_fast_pa_t_kernel(tc, x, out):
             )
             grouped_of[(b, m)] = grouped
 
-        def quantise_maps(b):
-            codes = packed.tile([P, MAPS, C], U32, align_bytes=64)
-            scales = packed.tile([P, MAPS, C], U8, align_bytes=64)
-            for m in range(MAPS):
+        def raise_rows(b):
+            up = raised[b % len(raised)]
+            nc.sync.dma_start(out=up[0:SHIFTED_P, :], in_=grouped_of[(b, CENTER)][BLOCK_P:P, :])
+            grouped_of[(b, UP)] = up
+
+        def quantise(b, maps):
+            if b not in codes_of:
+                codes = packed.tile([P, MAPS, C], U32, align_bytes=64)
+                scales = packed.tile([P, MAPS, C], U8, align_bytes=64)
+                codes_of[b] = codes
+                scales_of[b] = scales
+            for m in maps:
                 nc.vector.quantize_mx(
-                    out=codes[:, m, :].bitcast(FP8X4), scales=scales[:, m, :], in_=grouped_of[(b, m)][:]
+                    out=codes_of[b][:, m, :].bitcast(FP8X4), scales=scales_of[b][:, m, :], in_=grouped_of[(b, m)][:]
                 )
-            edge = edges[b % len(edges)]
+
+        def copy_edge(b):
             nc.sync.dma_start(
-                out=edge[0:BLOCK_P, :].bitcast(I32), in_=codes[0:BLOCK_P, CENTER, :].bitcast(I32)
+                out=edges[b % len(edges)][0:BLOCK_P, :].bitcast(I32),
+                in_=codes_of[b][0:BLOCK_P, CENTER, :].bitcast(I32),
             )
-            codes_of[b] = codes
-            scales_of[b] = scales
 
         def in_output_order(sums):
             return sums[:].rearrange("p h (g m) -> p h m g", g=HALVES)
@@ -154,83 +184,115 @@ def tile_cofeature_fast_pa_t_kernel(tc, x, out):
                 accum_out=partial_of[b][:, o : o + 1],
             )
             sums_of[(b, o)] = sums
-            if o < N_OFF - KEPT:
-                result = results.tile([P, HALVES * C], F32)
-                nc.vector.tensor_copy(
-                    out=result[:].rearrange("p (h m g) -> p h m g", h=HALVES, g=HALVES), in_=in_output_order(sums)
-                )
-                result_of[(b, o)] = result
+
+        def unload(b, o):
+            result = results.tile([P, HALVES * C], F32)
+            nc.vector.tensor_copy(
+                out=result[:].rearrange("p (h m g) -> p h m g", h=HALVES, g=HALVES),
+                in_=in_output_order(sums_of[(b, o)]),
+            )
+            result_of[(b, o)] = result
 
         def store(b, o, result):
             nc.sync.dma_start(out=out[b, o].rearrange("(p f) -> p f", p=P), in_=result[:])
 
-        def normalise_and_store(b, first, end):
-            these = slice(first, end)
-            total = psum_n.tile([P, N_OFF], F32)
-            nc.tensor.matmul(out=total[:, these], lhsT=ones[:], rhs=partial_of[b][:, these], start=True, stop=True)
-            norm = small.tile([P, N_OFF], F32)
-            nc.scalar.sqrt(out=norm[:, these], in_=total[:, these])
+        def total(b, offsets):
+            these = slice(min(offsets), max(offsets) + 1)
+            summed = psum_n.tile([P, N_OFF], F32)
+            nc.tensor.matmul(out=summed[:, these], lhsT=ones[:], rhs=partial_of[b][:, these], start=True, stop=True)
             floored = small.tile([P, N_OFF], F32)
-            nc.vector.tensor_scalar_max(out=floored[:, these], in0=norm[:, these], scalar1=EPS)
+            nc.vector.tensor_scalar_max(out=floored[:, these], in0=summed[:, these], scalar1=EPS * EPS)
+            floored_of[b] = floored
+
+        def root(b, offsets):
+            these = slice(min(offsets), max(offsets) + 1)
+            norm = small.tile([P, N_OFF], F32)
+            nc.scalar.sqrt(out=norm[:, these], in_=floored_of[b][:, these])
+            norm_of[b] = norm
+
+        def scale_and_store(b, offsets):
+            these = slice(min(offsets), max(offsets) + 1)
             inverse = small.tile([P, N_OFF], F32)
-            nc.vector.reciprocal(out=inverse[:, these], in_=floored[:, these])
-            for o in range(max(first, N_OFF - KEPT), end):
-                result = results.tile([P, HALVES * C], F32)
-                nc.vector.tensor_scalar_mul(
-                    out=result[:].rearrange("p (h m g) -> p h m g", h=HALVES, g=HALVES),
-                    in0=in_output_order(sums_of[(b, o)]),
-                    scalar1=inverse[:, o : o + 1],
-                )
-                store(b, o, result)
-            for o in range(first, min(end, N_OFF - KEPT)):
-                result = result_of[(b, o)]
-                factor = inverse[:, o : o + 1]
-                if b == B - 1 and end == N_OFF:
-                    nc.scalar.activation(out=result[:], in_=result[:], func=COPY, scale=factor)
-                else:
-                    nc.gpsimd.tensor_scalar(
-                        out=result[:], in0=result[:], scalar1=factor, scalar2=0.0, op0=MULT, op1=ADD
+            nc.vector.reciprocal(out=inverse[:, these], in_=norm_of[b][:, these])
+            for o in offsets:
+                if o in ORDER[-KEPT:]:
+                    result = results.tile([P, HALVES * C], F32)
+                    nc.vector.tensor_scalar_mul(
+                        out=result[:].rearrange("p (h m g) -> p h m g", h=HALVES, g=HALVES),
+                        in0=in_output_order(sums_of[(b, o)]),
+                        scalar1=inverse[:, o : o + 1],
                     )
-                store(b, o, result)
+                    store(b, o, result)
+            for o in offsets:
+                if o not in ORDER[-KEPT:]:
+                    result = result_of[(b, o)]
+                    factor = inverse[:, o : o + 1]
+                    if b == B - 1 and ORDER[-1] in offsets:
+                        nc.scalar.activation(out=result[:], in_=result[:], func=COPY, scale=factor)
+                    else:
+                        nc.gpsimd.tensor_scalar(
+                            out=result[:], in0=result[:], scalar1=factor, scalar2=0.0, op0=MULT, op1=ADD
+                        )
+                    store(b, o, result)
 
         for b in range(LOADS_AHEAD):
             load(b)
         for b in range(AHEAD):
-            replicate_border(b)
-            for n, m in enumerate([CENTER, UP, LEFT, RIGHT]):
+            replicate_border(b, copy_on_vector if b == 0 else copy_on_gpsimd)
+            for m in (CENTER, LEFT, RIGHT):
                 transpose_map(b, m)
-                copy_out(b, m, on_vector=(n % 2 == 1))
-            if b < AHEAD - 1:
-                quantise_maps(b)
-        replicate_border(AHEAD)
-        replicate_border(AHEAD + 1)
+                copy_out(b, m, on_vector=(m == LEFT))
+                if m == CENTER:
+                    raise_rows(b)
+            if b == 0:
+                quantise(b, [CENTER, LEFT, RIGHT])
+                copy_edge(b)
+        quantise(0, [UP])
+        replicate_border(AHEAD, copy_on_gpsimd)
+        replicate_border(AHEAD + 1, copy_on_gpsimd)
         for b in range(B):
             turning = b + AHEAD
+            partial = small.tile([P, N_OFF], F32)
+            partial_of[b] = partial
+            product(b, ORDER[0])
+            if b + 1 < B:
+                quantise(b + 1, [CENTER])
+                copy_edge(b + 1)
+                quantise(b + 1, [LEFT, RIGHT])
+            product(b, ORDER[1])
+            if b > 0:
+                total(b - 1, range(N_OFF))
+            if b + 1 < B:
+                quantise(b + 1, [UP])
+            if b > 0:
+                root(b - 1, range(N_OFF))
+            unload(b, ORDER[0])
             if turning < B:
-                transpose_map(turning, LEFT)
                 transpose_map(turning, CENTER)
-                transpose_map(turning, RIGHT)
-                copy_out(turning, LEFT, on_vector=False)
                 copy_out(turning, CENTER, on_vector=False)
-            if turning - 1 < B:
-                quantise_maps(turning - 1)
+                raise_rows(turning)
             if b + LOADS_AHEAD < B:
                 load(b + LOADS_AHEAD)
             if b > 0:
-                normalise_and_store(b - 1, 0, N_OFF)
-            if turning + 2 < B:
-                replicate_border(turning + 2)
-            partial = small.tile([P, N_OFF], F32)
-            partial_of[b] = partial
-            product(b, 0)
-            product(b, 1)
+                scale_and_store(b - 1, range(N_OFF))
+            unload(b, ORDER[1])
+            product(b, ORDER[2])
             if turning < B:
+                transpose_map(turning, LEFT)
+                copy_out(turning, LEFT, on_vector=False)
+            unload(b, ORDER[2])
+            product(b, ORDER[3])
+            if turning < B:
+                transpose_map(turning, RIGHT)
                 copy_out(turning, RIGHT, on_vector=False)
-                transpose_map(turning, UP)
-                copy_out(turning, UP, on_vector=True)
-            product(b, 2)
+            unload(b, ORDER[3])
             if b == B - 1:
-                normalise_and_store(b, 0, 3)
-            product(b, 3)
-            product(b, 4)
-        normalise_and_store(B - 1, 3, N_OFF)
+                total(b, ORDER[0:2])
+                root(b, ORDER[0:2])
+                scale_and_store(b, ORDER[0:2])
+            product(b, ORDER[4])
+            if turning + 2 < B:
+                replicate_border(turning + 2, copy_on_gpsimd)
+        total(B - 1, ORDER[2:])
+        root(B - 1, ORDER[2:])
+        scale_and_store(B - 1, ORDER[2:])

@@ -66,8 +66,9 @@ def tile_cofeature_fast_pa_t_kernel(tc, x, out):
             nc.vector.memset(up[:].bitcast(I32), 0)
             raised.append(up)
 
+        pixels = x.rearrange("b c i j -> (b c i j)")
         image = {}
-        ends_of = {}
+        starts_of = {}
         turned_of = {}
         grouped_of = {}
         codes_of = {}
@@ -80,11 +81,18 @@ def tile_cofeature_fast_pa_t_kernel(tc, x, out):
 
         def load(b):
             x_sb = images.tile([P, HALVES * K], BF16)
-            left = images.tile([P, HALVES * K], BF16)
-            pair = x[b].rearrange("(p h) i j -> p (h i j)", h=HALVES)
-            nc.sync.dma_start(out=x_sb[:], in_=pair)
-            nc.sync.dma_start(out=left[:, 1 : HALVES * K], in_=pair[:, 0 : HALVES * K - 1])
-            image[b] = (x_sb, left)
+            right = images.tile([P, HALVES * K], BF16)
+            nc.sync.dma_start(out=x_sb[:], in_=x[b].rearrange("(p h) i j -> p (h i j)", h=HALVES))
+            first = b * C * K + 1
+            run = HALVES * K
+            if b < B - 1:
+                nc.sync.dma_start(
+                    out=right[:], in_=pixels[first : first + P * run].rearrange("(p f) -> p f", p=P)
+                )
+            else:
+                pair = x[b].rearrange("(p h) i j -> p (h i j)", h=HALVES)
+                nc.sync.dma_start(out=right[:, 0 : run - 1], in_=pair[:, 1:run])
+            image[b] = (x_sb, right)
 
         def copy_on_gpsimd(dst, src):
             nc.gpsimd.tensor_scalar(out=dst, in0=src, scalar1=1.0, scalar2=0.0, op0=MULT, op1=ADD)
@@ -93,30 +101,29 @@ def tile_cofeature_fast_pa_t_kernel(tc, x, out):
             nc.vector.tensor_copy(out=dst, in_=src)
 
         def replicate_border(b, copy):
-            x_sb, left = image[b]
+            x_sb, right = image[b]
             rows = x_sb[:].rearrange("p (r j) -> p r j", j=W)
-            copy(left[:].rearrange("p (r j) -> p r j", j=W)[:, :, 0:1], rows[:, :, 0:1])
-            ends = planes.tile([P, HALVES, P, 2], BF16)
-            by_row = ends[:].rearrange("p h (i q) e -> p (h i) q e", q=BLOCK_P)
+            copy(right[:].rearrange("p (r j) -> p r j", j=W)[:, :, W - 1 : W], rows[:, :, W - 1 : W])
+            starts = planes.tile([P, HALVES, P, 2], BF16)
+            by_row = starts[:].rearrange("p h (i q) e -> p (h i) q e", q=BLOCK_P)
             copy(
-                by_row[:, :, 0 : BLOCK_P - 1, :],
+                by_row[:, :, 1:BLOCK_P, :],
                 rows[:, :, PACK - 1 : W - 1].rearrange("p r (q t) -> p r q t", t=PACK)[:, :, :, 0:2],
             )
-            copy(by_row[:, :, BLOCK_P - 1, :], rows[:, :, W - 1 : W].to_broadcast([P, HALVES * H, 2]))
-            ends_of[b] = ends
+            copy(by_row[:, :, 0, :], rows[:, :, 0:1].to_broadcast([P, HALVES * H, 2]))
+            starts_of[b] = starts
 
         def transpose_map(b, m):
-            x_sb, left = image[b]
             words_of = [
-                source[:].bitcast(F32).rearrange("p (h w u) -> p h u w", h=HALVES, u=2) for source in (x_sb, left)
+                source[:].bitcast(F32).rearrange("p (h w u) -> p h u w", h=HALVES, u=2) for source in image[b]
             ]
             turned = psum_t.tile([P, HALVES, 2, P], F32)
             for h in range(HALVES):
-                ends = ends_of[b][:, h].rearrange("p m e -> p (m e)").bitcast(F32)
+                starts = starts_of[b][:, h].rearrange("p m e -> p (m e)").bitcast(F32)
                 words = {
                     CENTER: [words_of[0][:, h, 0, :], words_of[0][:, h, 1, :]],
-                    LEFT: [words_of[1][:, h, 0, :], words_of[1][:, h, 1, :]],
-                    RIGHT: [words_of[1][:, h, 1, :], ends],
+                    LEFT: [starts, words_of[1][:, h, 0, :]],
+                    RIGHT: [words_of[1][:, h, 0, :], words_of[1][:, h, 1, :]],
                 }[m]
                 for u in range(2):
                     nc.tensor.transpose(turned[:, h, u, :], words[u], identity[:])

@@ -28,9 +28,11 @@ MAPS = 4
 OFFSETS = [(LEFT, True), (CENTER, True), (RIGHT, True), (LEFT, False), (CENTER, False)]
 N_OFF = len(OFFSETS)
 ORDER = [3, 4, 0, 1, 2]
+STORES = [[2], [3, 4], [0, 1]]
 KEPT = 1
 AHEAD = 2
-LOADS_AHEAD = 6
+LOADS = [(0, 1), (1, 1)] + [(b, 2) for b in range(2, B, 2)]
+FIRST_LOADS = 4
 
 FLOPS = 2 * B * N_OFF * C * C * K
 
@@ -39,12 +41,11 @@ def tile_cofeature_fast_pa_t_kernel(tc, x, out):
     nc = tc.nc
     with ExitStack() as ctx:
         const = ctx.enter_context(tc.tile_pool(name="const", bufs=1))
-        images = ctx.enter_context(tc.tile_pool(name="images", bufs=B))
         stage = ctx.enter_context(tc.tile_pool(name="stage", bufs=3 * (MAPS - 1)))
         packed = ctx.enter_context(tc.tile_pool(name="packed", bufs=3))
         planes = ctx.enter_context(tc.tile_pool(name="planes", bufs=AHEAD + 2))
         small = ctx.enter_context(tc.tile_pool(name="small", bufs=3))
-        results = ctx.enter_context(tc.tile_pool(name="results", bufs=4 * N_OFF))
+        results = ctx.enter_context(tc.tile_pool(name="results", bufs=3 * len(STORES)))
         psum_t = ctx.enter_context(tc.psum_pool(name="psum_t", bufs=2))
         psum_g = ctx.enter_context(tc.psum_pool(name="psum_g", bufs=5))
         psum_n = ctx.enter_context(tc.psum_pool(name="psum_n", bufs=1))
@@ -66,9 +67,8 @@ def tile_cofeature_fast_pa_t_kernel(tc, x, out):
             nc.vector.memset(up[:].bitcast(I32), 0)
             raised.append(up)
 
-        pixels = x.rearrange("b c i j -> (b c i j)")
         image = {}
-        starts_of = {}
+        planes_of = {}
         turned_of = {}
         grouped_of = {}
         codes_of = {}
@@ -78,21 +78,16 @@ def tile_cofeature_fast_pa_t_kernel(tc, x, out):
         floored_of = {}
         norm_of = {}
         result_of = {}
+        stored_of = {}
 
-        def load(b):
-            x_sb = images.tile([P, HALVES * K], BF16)
-            right = images.tile([P, HALVES * K], BF16)
-            nc.sync.dma_start(out=x_sb[:], in_=x[b].rearrange("(p h) i j -> p (h i j)", h=HALVES))
-            first = b * C * K + 1
-            run = HALVES * K
-            if b < B - 1:
-                nc.sync.dma_start(
-                    out=right[:], in_=pixels[first : first + P * run].rearrange("(p f) -> p f", p=P)
-                )
-            else:
-                pair = x[b].rearrange("(p h) i j -> p (h i j)", h=HALVES)
-                nc.sync.dma_start(out=right[:, 0 : run - 1], in_=pair[:, 1:run])
-            image[b] = (x_sb, right)
+        def load(n):
+            first, count = LOADS[n]
+            x_sb = const.tile([P, count, HALVES * K], BF16, name="x%d" % first)
+            nc.sync.dma_start(
+                out=x_sb[:], in_=x[first : first + count].rearrange("b (p h) i j -> p b (h i j)", h=HALVES)
+            )
+            for e in range(count):
+                image[first + e] = x_sb[:, e, :]
 
         def copy_on_gpsimd(dst, src):
             nc.gpsimd.tensor_scalar(out=dst, in0=src, scalar1=1.0, scalar2=0.0, op0=MULT, op1=ADD)
@@ -100,33 +95,31 @@ def tile_cofeature_fast_pa_t_kernel(tc, x, out):
         def copy_on_vector(dst, src):
             nc.vector.tensor_copy(out=dst, in_=src)
 
-        def replicate_border(b, copy):
-            x_sb, right = image[b]
-            rows = x_sb[:].rearrange("p (r j) -> p r j", j=W)
-            copy(right[:].rearrange("p (r j) -> p r j", j=W)[:, :, W - 1 : W], rows[:, :, W - 1 : W])
-            starts = planes.tile([P, HALVES, P, 2], BF16)
-            by_row = starts[:].rearrange("p h (i q) e -> p (h i) q e", q=BLOCK_P)
-            copy(
-                by_row[:, :, 1:BLOCK_P, :],
-                rows[:, :, PACK - 1 : W - 1].rearrange("p r (q t) -> p r q t", t=PACK)[:, :, :, 0:2],
+        def shift_columns(b, copy):
+            words = planes.tile([P, 3, HALVES, P, 2], BF16)
+            rows = image[b].rearrange("p (r j) -> p r j", j=W)
+            inner = rows[:, :, PACK - 1 : W - 1].rearrange("p r (q t) -> p r q t", t=PACK)[:, :, :, 0:2]
+            before, after = [words[:, n].rearrange("p h (i q) e -> p (h i) q e", q=BLOCK_P) for n in (0, 2)]
+            copy_on_vector(
+                words[:, 1].rearrange("p h m e -> p (h m) e"),
+                image[b].rearrange("p (w t) -> p w t", t=PACK)[:, :, 1:3],
             )
-            copy(by_row[:, :, 0, :], rows[:, :, 0:1].to_broadcast([P, HALVES * H, 2]))
-            starts_of[b] = starts
+            copy(before[:, :, 1:BLOCK_P, :], inner)
+            copy(before[:, :, 0, :], rows[:, :, 0:1].to_broadcast([P, HALVES * H, 2]))
+            copy(after[:, :, 0 : BLOCK_P - 1, :], inner)
+            copy(after[:, :, BLOCK_P - 1, :], rows[:, :, W - 1 : W].to_broadcast([P, HALVES * H, 2]))
+            planes_of[b] = words
 
         def transpose_map(b, m):
-            words_of = [
-                source[:].bitcast(F32).rearrange("p (h w u) -> p h u w", h=HALVES, u=2) for source in image[b]
-            ]
             turned = psum_t.tile([P, HALVES, 2, P], F32)
             for h in range(HALVES):
-                starts = starts_of[b][:, h].rearrange("p m e -> p (m e)").bitcast(F32)
-                words = {
-                    CENTER: [words_of[0][:, h, 0, :], words_of[0][:, h, 1, :]],
-                    LEFT: [starts, words_of[1][:, h, 0, :]],
-                    RIGHT: [words_of[1][:, h, 0, :], words_of[1][:, h, 1, :]],
-                }[m]
                 for u in range(2):
-                    nc.tensor.transpose(turned[:, h, u, :], words[u], identity[:])
+                    if m == CENTER:
+                        words = image[b].bitcast(F32).rearrange("p (h w u) -> p h u w", h=HALVES, u=2)[:, h, u, :]
+                    else:
+                        plane = u if m == LEFT else u + 1
+                        words = planes_of[b][:, plane, h].rearrange("p m e -> p (m e)").bitcast(F32)
+                    nc.tensor.transpose(turned[:, h, u, :], words, identity[:])
             turned_of[(b, m)] = turned
 
         def copy_out(b, m, on_vector):
@@ -193,15 +186,25 @@ def tile_cofeature_fast_pa_t_kernel(tc, x, out):
             sums_of[(b, o)] = sums
 
         def unload(b, o):
-            result = results.tile([P, HALVES * C], F32)
             nc.vector.tensor_copy(
-                out=result[:].rearrange("p (h m g) -> p h m g", h=HALVES, g=HALVES),
+                out=result_tile(b, o).rearrange("p (h m g) -> p h m g", h=HALVES, g=HALVES),
                 in_=in_output_order(sums_of[(b, o)]),
             )
-            result_of[(b, o)] = result
 
-        def store(b, o, result):
-            nc.sync.dma_start(out=out[b, o].rearrange("(p f) -> p f", p=P), in_=result[:])
+        def result_tile(b, o):
+            if (b, o) not in result_of:
+                group = [g for g in STORES if o in g][0]
+                results_sb = results.tile([P, len(group), HALVES * C], F32)
+                for n, member in enumerate(group):
+                    result_of[(b, member)] = results_sb[:, n, :]
+                stored_of[(b, group[0])] = results_sb
+            return result_of[(b, o)]
+
+        def store(b, group):
+            nc.sync.dma_start(
+                out=out[b, group[0] : group[-1] + 1].rearrange("o (p f) -> p o f", p=P),
+                in_=stored_of[(b, group[0])][:],
+            )
 
         def total(b, offsets):
             these = slice(min(offsets), max(offsets) + 1)
@@ -223,29 +226,27 @@ def tile_cofeature_fast_pa_t_kernel(tc, x, out):
             nc.vector.reciprocal(out=inverse[:, these], in_=norm_of[b][:, these])
             for o in offsets:
                 if o in ORDER[-KEPT:]:
-                    result = results.tile([P, HALVES * C], F32)
                     nc.vector.tensor_scalar_mul(
-                        out=result[:].rearrange("p (h m g) -> p h m g", h=HALVES, g=HALVES),
+                        out=result_tile(b, o).rearrange("p (h m g) -> p h m g", h=HALVES, g=HALVES),
                         in0=in_output_order(sums_of[(b, o)]),
                         scalar1=inverse[:, o : o + 1],
                     )
-                    store(b, o, result)
-            for o in offsets:
-                if o not in ORDER[-KEPT:]:
-                    result = result_of[(b, o)]
+            for o in ORDER[:-KEPT]:
+                if o in offsets:
+                    result = result_tile(b, o)
                     factor = inverse[:, o : o + 1]
                     if b == B - 1 and ORDER[-1] in offsets:
-                        nc.scalar.activation(out=result[:], in_=result[:], func=COPY, scale=factor)
+                        nc.scalar.activation(out=result, in_=result, func=COPY, scale=factor)
                     else:
-                        nc.gpsimd.tensor_scalar(
-                            out=result[:], in0=result[:], scalar1=factor, scalar2=0.0, op0=MULT, op1=ADD
-                        )
-                    store(b, o, result)
+                        nc.gpsimd.tensor_scalar(out=result, in0=result, scalar1=factor, scalar2=0.0, op0=MULT, op1=ADD)
+            for group in STORES:
+                if group[0] in offsets:
+                    store(b, group)
 
-        for b in range(LOADS_AHEAD):
-            load(b)
+        for n in range(FIRST_LOADS):
+            load(n)
         for b in range(AHEAD):
-            replicate_border(b, copy_on_vector if b == 0 else copy_on_gpsimd)
+            shift_columns(b, copy_on_vector if b == 0 else copy_on_gpsimd)
             for m in (CENTER, LEFT, RIGHT):
                 transpose_map(b, m)
                 copy_out(b, m, on_vector=(m == LEFT))
@@ -255,8 +256,8 @@ def tile_cofeature_fast_pa_t_kernel(tc, x, out):
                 quantise(b, [CENTER, LEFT, RIGHT])
                 copy_edge(b)
         quantise(0, [UP])
-        replicate_border(AHEAD, copy_on_gpsimd)
-        replicate_border(AHEAD + 1, copy_on_gpsimd)
+        shift_columns(AHEAD, copy_on_gpsimd)
+        shift_columns(AHEAD + 1, copy_on_gpsimd)
         for b in range(B):
             turning = b + AHEAD
             partial = small.tile([P, N_OFF], F32)
@@ -278,8 +279,8 @@ def tile_cofeature_fast_pa_t_kernel(tc, x, out):
                 transpose_map(turning, CENTER)
                 copy_out(turning, CENTER, on_vector=False)
                 raise_rows(turning)
-            if b + LOADS_AHEAD < B:
-                load(b + LOADS_AHEAD)
+            if b % 2 == 0 and FIRST_LOADS + b // 2 < len(LOADS):
+                load(FIRST_LOADS + b // 2)
             if b > 0:
                 scale_and_store(b - 1, range(N_OFF))
             unload(b, ORDER[1])
@@ -299,7 +300,7 @@ def tile_cofeature_fast_pa_t_kernel(tc, x, out):
                 scale_and_store(b, ORDER[0:2])
             product(b, ORDER[4])
             if turning + 2 < B:
-                replicate_border(turning + 2, copy_on_gpsimd)
+                shift_columns(turning + 2, copy_on_gpsimd)
         total(B - 1, ORDER[2:])
         root(B - 1, ORDER[2:])
         scale_and_store(B - 1, ORDER[2:])

@@ -28,8 +28,8 @@ MAPS = 4
 OFFSETS = [(LEFT, True), (CENTER, True), (RIGHT, True), (LEFT, False), (CENTER, False)]
 N_OFF = len(OFFSETS)
 ORDER = [3, 4, 0, 1, 2]
-STORES = [[2], [3, 4], [0, 1]]
-KEPT = 1
+STORES = [[0, 1], [2], [3, 4]]
+KEPT = 3
 AHEAD = 2
 LOADS = [(0, 1), (1, 1)] + [(b, 2) for b in range(2, B, 2)]
 FIRST_LOADS = 4
@@ -47,8 +47,7 @@ def tile_cofeature_fast_pa_t_kernel(tc, x, out):
         small = ctx.enter_context(tc.tile_pool(name="small", bufs=3))
         results = ctx.enter_context(tc.tile_pool(name="results", bufs=3 * len(STORES)))
         psum_t = ctx.enter_context(tc.psum_pool(name="psum_t", bufs=2))
-        psum_g = ctx.enter_context(tc.psum_pool(name="psum_g", bufs=5))
-        psum_n = ctx.enter_context(tc.psum_pool(name="psum_n", bufs=1))
+        psum_g = ctx.enter_context(tc.psum_pool(name="psum_g", bufs=6))
         ctx.enter_context(tc.manual_schedule())
 
         identity = const.tile([P, P], F32)
@@ -208,7 +207,8 @@ def tile_cofeature_fast_pa_t_kernel(tc, x, out):
 
         def total(b, offsets):
             these = slice(min(offsets), max(offsets) + 1)
-            summed = psum_n.tile([P, N_OFF], F32)
+            turned = psum_t.tile([P, HALVES, 2, P], F32)
+            summed = turned[:, 0, 0, 0:N_OFF]
             nc.tensor.matmul(out=summed[:, these], lhsT=ones[:], rhs=partial_of[b][:, these], start=True, stop=True)
             floored = small.tile([P, N_OFF], F32)
             nc.vector.tensor_scalar_max(out=floored[:, these], in0=summed[:, these], scalar1=EPS * EPS)
@@ -288,12 +288,10 @@ def tile_cofeature_fast_pa_t_kernel(tc, x, out):
             if turning < B:
                 transpose_map(turning, LEFT)
                 copy_out(turning, LEFT, on_vector=False)
-            unload(b, ORDER[2])
             product(b, ORDER[3])
             if turning < B:
                 transpose_map(turning, RIGHT)
                 copy_out(turning, RIGHT, on_vector=False)
-            unload(b, ORDER[3])
             if b == B - 1:
                 total(b, ORDER[0:2])
                 root(b, ORDER[0:2])

@@ -43,7 +43,7 @@ def tile_cofeature_fast_pa_t_kernel(tc, x, out):
         const = ctx.enter_context(tc.tile_pool(name="const", bufs=1))
         stage = ctx.enter_context(tc.tile_pool(name="stage", bufs=3 * (MAPS - 1)))
         packed = ctx.enter_context(tc.tile_pool(name="packed", bufs=3))
-        planes = ctx.enter_context(tc.tile_pool(name="planes", bufs=AHEAD + 2))
+        planes = ctx.enter_context(tc.tile_pool(name="planes", bufs=AHEAD + 3))
         small = ctx.enter_context(tc.tile_pool(name="small", bufs=3))
         results = ctx.enter_context(tc.tile_pool(name="results", bufs=3 * len(STORES)))
         psum_t = ctx.enter_context(tc.psum_pool(name="psum_t", bufs=2))
@@ -67,7 +67,8 @@ def tile_cofeature_fast_pa_t_kernel(tc, x, out):
             raised.append(up)
 
         image = {}
-        planes_of = {}
+        inner_of = {}
+        seams_of = {}
         turned_of = {}
         grouped_of = {}
         codes_of = {}
@@ -76,6 +77,7 @@ def tile_cofeature_fast_pa_t_kernel(tc, x, out):
         sums_of = {}
         floored_of = {}
         norm_of = {}
+        inverse_of = {}
         result_of = {}
         stored_of = {}
 
@@ -94,20 +96,29 @@ def tile_cofeature_fast_pa_t_kernel(tc, x, out):
         def copy_on_vector(dst, src):
             nc.vector.tensor_copy(out=dst, in_=src)
 
-        def shift_columns(b, copy):
-            words = planes.tile([P, 3, HALVES, P, 2], BF16)
-            rows = image[b].rearrange("p (r j) -> p r j", j=W)
-            inner = rows[:, :, PACK - 1 : W - 1].rearrange("p r (q t) -> p r q t", t=PACK)[:, :, :, 0:2]
-            before, after = [words[:, n].rearrange("p h (i q) e -> p (h i) q e", q=BLOCK_P) for n in (0, 2)]
+        def shift_inner(b):
+            inner = planes.tile([P, HALVES, P, 2], BF16)
             copy_on_vector(
-                words[:, 1].rearrange("p h m e -> p (h m) e"),
+                inner[:].rearrange("p h m e -> p (h m) e"),
                 image[b].rearrange("p (w t) -> p w t", t=PACK)[:, :, 1:3],
             )
-            copy(before[:, :, 1:BLOCK_P, :], inner)
-            copy(before[:, :, 0, :], rows[:, :, 0:1].to_broadcast([P, HALVES * H, 2]))
-            copy(after[:, :, 0 : BLOCK_P - 1, :], inner)
-            copy(after[:, :, BLOCK_P - 1, :], rows[:, :, W - 1 : W].to_broadcast([P, HALVES * H, 2]))
-            planes_of[b] = words
+            inner_of[b] = inner
+
+        def shift_seams(b, copy):
+            seams = planes.tile([P, (HALVES * H + 1) * W // 2], BF16)
+            rows = image[b].rearrange("p (r j) -> p r j", j=W)
+            words = seams[:, 0 : HALVES * P * 2].rearrange("p (r q e) -> p r q e", q=BLOCK_P, e=2)
+            copy(
+                words[:, :, 1:BLOCK_P, :],
+                rows[:, :, PACK - 1 : W - 1].rearrange("p r (q t) -> p r q t", t=PACK)[:, :, :, 0:2],
+            )
+            copy(words[:, :, 0, :], rows[:, :, 0:1].to_broadcast([P, HALVES * H, 2]))
+            seams_of[b] = seams
+
+        def replace_borders(b, copy):
+            words = seams_of[b][:, W // 2 :].rearrange("p (r v) -> p r v", v=W // 2)
+            rows = image[b].rearrange("p (r j) -> p r j", j=W)
+            copy(words[:, :, 0:2], rows[:, :, W - 1 : W].to_broadcast([P, HALVES * H, 2]))
 
         def transpose_map(b, m):
             turned = psum_t.tile([P, HALVES, 2, P], F32)
@@ -115,9 +126,11 @@ def tile_cofeature_fast_pa_t_kernel(tc, x, out):
                 for u in range(2):
                     if m == CENTER:
                         words = image[b].bitcast(F32).rearrange("p (h w u) -> p h u w", h=HALVES, u=2)[:, h, u, :]
+                    elif (m == LEFT) == (u == 1):
+                        words = inner_of[b][:, h].rearrange("p m e -> p (m e)").bitcast(F32)
                     else:
-                        plane = u if m == LEFT else u + 1
-                        words = planes_of[b][:, plane, h].rearrange("p m e -> p (m e)").bitcast(F32)
+                        start = h * P + (1 if m == RIGHT else 0)
+                        words = seams_of[b][:].bitcast(F32)[:, start : start + P]
                     nc.tensor.transpose(turned[:, h, u, :], words, identity[:])
             turned_of[(b, m)] = turned
 
@@ -175,14 +188,16 @@ def tile_cofeature_fast_pa_t_kernel(tc, x, out):
                         start=(n == 0),
                         stop=(n == len(stationary) - 1),
                     )
+            sums_of[(b, o)] = sums
+
+        def square(b, o):
             squared = small.tile([P, HALVES * C], F32)
             nc.scalar.activation(
                 out=squared[:],
-                in_=sums[:].rearrange("p h d -> p (h d)"),
+                in_=sums_of[(b, o)][:].rearrange("p h d -> p (h d)"),
                 func=SQUARE,
                 accum_out=partial_of[b][:, o : o + 1],
             )
-            sums_of[(b, o)] = sums
 
         def unload(b, o):
             nc.vector.tensor_copy(
@@ -199,11 +214,13 @@ def tile_cofeature_fast_pa_t_kernel(tc, x, out):
                 stored_of[(b, group[0])] = results_sb
             return result_of[(b, o)]
 
-        def store(b, group):
-            nc.sync.dma_start(
-                out=out[b, group[0] : group[-1] + 1].rearrange("o (p f) -> p o f", p=P),
-                in_=stored_of[(b, group[0])][:],
-            )
+        def store(b, offsets):
+            for group in STORES:
+                if group[0] in offsets:
+                    nc.sync.dma_start(
+                        out=out[b, group[0] : group[-1] + 1].rearrange("o (p f) -> p o f", p=P),
+                        in_=stored_of[(b, group[0])][:],
+                    )
 
         def total(b, offsets):
             these = slice(min(offsets), max(offsets) + 1)
@@ -220,61 +237,70 @@ def tile_cofeature_fast_pa_t_kernel(tc, x, out):
             nc.scalar.sqrt(out=norm[:, these], in_=floored_of[b][:, these])
             norm_of[b] = norm
 
-        def scale_and_store(b, offsets):
+        def invert(b, offsets):
             these = slice(min(offsets), max(offsets) + 1)
             inverse = small.tile([P, N_OFF], F32)
             nc.vector.reciprocal(out=inverse[:, these], in_=norm_of[b][:, these])
-            for o in offsets:
-                if o in ORDER[-KEPT:]:
-                    nc.vector.tensor_scalar_mul(
-                        out=result_tile(b, o).rearrange("p (h m g) -> p h m g", h=HALVES, g=HALVES),
-                        in0=in_output_order(sums_of[(b, o)]),
-                        scalar1=inverse[:, o : o + 1],
-                    )
-            for o in ORDER[:-KEPT]:
-                if o in offsets:
-                    result = result_tile(b, o)
-                    factor = inverse[:, o : o + 1]
-                    if b == B - 1 and ORDER[-1] in offsets:
-                        nc.scalar.activation(out=result, in_=result, func=COPY, scale=factor)
-                    else:
-                        nc.gpsimd.tensor_scalar(out=result, in0=result, scalar1=factor, scalar2=0.0, op0=MULT, op1=ADD)
-            for group in STORES:
-                if group[0] in offsets:
-                    store(b, group)
+            inverse_of[b] = inverse
+
+        def scale_out(b, o, halves=(0, HALVES), on_vector=True):
+            these = slice(*halves)
+            result = result_tile(b, o).rearrange("p (h m g) -> p h m g", h=HALVES, g=HALVES)[:, these]
+            sums = in_output_order(sums_of[(b, o)])[:, these]
+            factor = inverse_of[b][:, o : o + 1]
+            if on_vector:
+                nc.vector.tensor_scalar_mul(out=result, in0=sums, scalar1=factor)
+            else:
+                nc.scalar.activation(out=result, in_=sums, func=COPY, scale=factor)
+
+        def scale_in_place(b, o):
+            result = result_tile(b, o)
+            factor = inverse_of[b][:, o : o + 1]
+            nc.gpsimd.tensor_scalar(out=result, in0=result, scalar1=factor, scalar2=0.0, op0=MULT, op1=ADD)
 
         for n in range(FIRST_LOADS):
             load(n)
         for b in range(AHEAD):
-            shift_columns(b, copy_on_vector if b == 0 else copy_on_gpsimd)
-            for m in (CENTER, LEFT, RIGHT):
-                transpose_map(b, m)
-                copy_out(b, m, on_vector=(m == LEFT))
-                if m == CENTER:
-                    raise_rows(b)
+            copy = copy_on_vector if b == 0 else copy_on_gpsimd
+            shift_inner(b)
+            shift_seams(b, copy)
+            transpose_map(b, CENTER)
+            copy_out(b, CENTER, on_vector=False)
+            raise_rows(b)
+            transpose_map(b, LEFT)
+            copy_out(b, LEFT, on_vector=True)
+            replace_borders(b, copy)
             if b == 0:
+                transpose_map(b, RIGHT)
+                copy_out(b, RIGHT, on_vector=False)
                 quantise(b, [CENTER, LEFT, RIGHT])
                 copy_edge(b)
         quantise(0, [UP])
-        shift_columns(AHEAD, copy_on_gpsimd)
-        shift_columns(AHEAD + 1, copy_on_gpsimd)
+        for b in (AHEAD, AHEAD + 1):
+            shift_inner(b)
+            shift_seams(b, copy_on_gpsimd)
         for b in range(B):
             turning = b + AHEAD
             partial = small.tile([P, N_OFF], F32)
             partial_of[b] = partial
             product(b, ORDER[0])
+            square(b, ORDER[0])
             if b + 1 < B:
                 quantise(b + 1, [CENTER])
                 copy_edge(b + 1)
-                quantise(b + 1, [LEFT, RIGHT])
+                quantise(b + 1, [LEFT])
+            if b > 0:
+                quantise(b, [RIGHT])
             product(b, ORDER[1])
+            square(b, ORDER[1])
             if b > 0:
                 total(b - 1, range(N_OFF))
             if b + 1 < B:
                 quantise(b + 1, [UP])
             if b > 0:
                 root(b - 1, range(N_OFF))
-            unload(b, ORDER[0])
+            if b < B - 1:
+                unload(b, ORDER[0])
             if turning < B:
                 transpose_map(turning, CENTER)
                 copy_out(turning, CENTER, on_vector=False)
@@ -282,23 +308,54 @@ def tile_cofeature_fast_pa_t_kernel(tc, x, out):
             if b % 2 == 0 and FIRST_LOADS + b // 2 < len(LOADS):
                 load(FIRST_LOADS + b // 2)
             if b > 0:
-                scale_and_store(b - 1, range(N_OFF))
+                invert(b - 1, range(N_OFF))
+                for o in ORDER[-KEPT:]:
+                    scale_out(b - 1, o)
+                for o in ORDER[:-KEPT]:
+                    scale_in_place(b - 1, o)
+                store(b - 1, range(N_OFF))
+            if b == B - 1:
+                break
             unload(b, ORDER[1])
             product(b, ORDER[2])
+            square(b, ORDER[2])
             if turning < B:
                 transpose_map(turning, LEFT)
                 copy_out(turning, LEFT, on_vector=False)
             product(b, ORDER[3])
-            if turning < B:
-                transpose_map(turning, RIGHT)
-                copy_out(turning, RIGHT, on_vector=False)
-            if b == B - 1:
-                total(b, ORDER[0:2])
-                root(b, ORDER[0:2])
-                scale_and_store(b, ORDER[0:2])
+            square(b, ORDER[3])
+            transpose_map(b + 1, RIGHT)
+            copy_out(b + 1, RIGHT, on_vector=False)
             product(b, ORDER[4])
+            square(b, ORDER[4])
+            if turning < B:
+                replace_borders(turning, copy_on_gpsimd)
             if turning + 2 < B:
-                shift_columns(turning + 2, copy_on_gpsimd)
-        total(B - 1, ORDER[2:])
-        root(B - 1, ORDER[2:])
-        scale_and_store(B - 1, ORDER[2:])
+                shift_inner(turning + 2)
+                shift_seams(turning + 2, copy_on_gpsimd)
+
+        b = B - 1
+        first, second, last = [3, 4], [0, 1], [2]
+        total(b, first)
+        root(b, first)
+        invert(b, first)
+        for o in first:
+            scale_out(b, o)
+        store(b, first)
+        for o in second:
+            product(b, o)
+            square(b, o)
+        product(b, last[0])
+        total(b, second)
+        square(b, last[0])
+        root(b, second)
+        invert(b, second)
+        total(b, last)
+        scale_out(b, second[0])
+        root(b, last)
+        scale_out(b, second[1], on_vector=False)
+        store(b, second)
+        invert(b, last)
+        scale_out(b, last[0], halves=(0, 1))
+        scale_out(b, last[0], halves=(1, 2), on_vector=False)
+        store(b, last)

@@ -22,9 +22,11 @@ HALVES = C // P
 PACK = 4
 BLOCK_P = 8
 SHIFTED_P = P - BLOCK_P
+GROUP_P = 32
+GROUP_ROWS = GROUP_P // BLOCK_P
 
-LEFT, CENTER, RIGHT, UP = 0, 1, 2, 3
-MAPS = 4
+LEFT, CENTER, RIGHT = 0, 1, 2
+MAPS = 3
 OFFSETS = [(LEFT, True), (CENTER, True), (RIGHT, True), (LEFT, False), (CENTER, False)]
 N_OFF = len(OFFSETS)
 ORDER = [3, 4, 0, 1, 2]
@@ -41,7 +43,7 @@ def tile_cofeature_fast_pa_t_kernel(tc, x, out):
     nc = tc.nc
     with ExitStack() as ctx:
         const = ctx.enter_context(tc.tile_pool(name="const", bufs=1))
-        stage = ctx.enter_context(tc.tile_pool(name="stage", bufs=3 * (MAPS - 1)))
+        stage = ctx.enter_context(tc.tile_pool(name="stage", bufs=3 * MAPS))
         packed = ctx.enter_context(tc.tile_pool(name="packed", bufs=3))
         planes = ctx.enter_context(tc.tile_pool(name="planes", bufs=AHEAD + 3))
         small = ctx.enter_context(tc.tile_pool(name="small", bufs=3))
@@ -58,13 +60,17 @@ def tile_cofeature_fast_pa_t_kernel(tc, x, out):
         nc.scalar.sqrt(out=warm[:], in_=ones[:, 0:1])
         edges = []
         raised = []
+        raised_scales = []
         for e in range(AHEAD + 1):
             edge = const.tile([P, C], U32, name="edge%d" % e, align_bytes=64)
             nc.vector.memset(edge[:].bitcast(I32), 0)
             edges.append(edge)
-            up = const.tile([P, C * PACK], BF16, name="up%d" % e, align_bytes=64)
+            up = const.tile([P, C], U32, name="up%d" % e, align_bytes=64)
             nc.vector.memset(up[:].bitcast(I32), 0)
             raised.append(up)
+            up_scales = const.tile([P, C], U8, name="up_scales%d" % e, align_bytes=64)
+            nc.vector.memset(up_scales[:].bitcast(I32), 0)
+            raised_scales.append(up_scales)
 
         image = {}
         inner_of = {}
@@ -144,9 +150,17 @@ def tile_cofeature_fast_pa_t_kernel(tc, x, out):
             grouped_of[(b, m)] = grouped
 
         def raise_rows(b):
-            up = raised[b % len(raised)]
-            nc.sync.dma_start(out=up[0:SHIFTED_P, :], in_=grouped_of[(b, CENTER)][BLOCK_P:P, :])
-            grouped_of[(b, UP)] = up
+            codes, scales = codes_of[b][:, CENTER, :], scales_of[b][:, CENTER, :]
+            up, up_scales = raised[b % len(raised)], raised_scales[b % len(raised)]
+            nc.sync.dma_start(out=up[0:SHIFTED_P, :].bitcast(I32), in_=codes[BLOCK_P:P, :].bitcast(I32))
+            for r in range(GROUP_ROWS - 1):
+                nc.sync.dma_start(
+                    out=up_scales[r:P:GROUP_P, :].bitcast(I32), in_=scales[r + 1 : P : GROUP_P, :].bitcast(I32)
+                )
+            nc.sync.dma_start(
+                out=up_scales[GROUP_ROWS - 1 : P - GROUP_P : GROUP_P, :].bitcast(I32),
+                in_=scales[GROUP_P:P:GROUP_P, :].bitcast(I32),
+            )
 
         def quantise(b, maps):
             if b not in codes_of:
@@ -170,12 +184,13 @@ def tile_cofeature_fast_pa_t_kernel(tc, x, out):
 
         def product(b, o):
             codes, scales, edge = codes_of[b], scales_of[b], edges[b % len(edges)]
+            up, up_scales = raised[b % len(raised)], raised_scales[b % len(raised)]
             m, row_above = OFFSETS[o]
             sums = psum_g.tile([P, HALVES, C], F32)
             for h in range(HALVES):
                 cols = slice(h * P, (h + 1) * P)
                 if row_above:
-                    stationary = [(codes[:, UP, cols], scales[:, UP, cols]), (edge[:, cols], scales[:, CENTER, cols])]
+                    stationary = [(up[:, cols], up_scales[:, cols]), (edge[:, cols], scales[:, CENTER, cols])]
                 else:
                     stationary = [(codes[:, CENTER, cols], scales[:, CENTER, cols])]
                 for n, (words, plane) in enumerate(stationary):
@@ -266,7 +281,6 @@ def tile_cofeature_fast_pa_t_kernel(tc, x, out):
             shift_seams(b, copy)
             transpose_map(b, CENTER)
             copy_out(b, CENTER, on_vector=False)
-            raise_rows(b)
             transpose_map(b, LEFT)
             copy_out(b, LEFT, on_vector=True)
             replace_borders(b, copy)
@@ -275,7 +289,7 @@ def tile_cofeature_fast_pa_t_kernel(tc, x, out):
                 copy_out(b, RIGHT, on_vector=False)
                 quantise(b, [CENTER, LEFT, RIGHT])
                 copy_edge(b)
-        quantise(0, [UP])
+                raise_rows(b)
         for b in (AHEAD, AHEAD + 1):
             shift_inner(b)
             shift_seams(b, copy_on_gpsimd)
@@ -288,6 +302,7 @@ def tile_cofeature_fast_pa_t_kernel(tc, x, out):
             if b + 1 < B:
                 quantise(b + 1, [CENTER])
                 copy_edge(b + 1)
+                raise_rows(b + 1)
                 quantise(b + 1, [LEFT])
             if b > 0:
                 quantise(b, [RIGHT])
@@ -295,8 +310,6 @@ def tile_cofeature_fast_pa_t_kernel(tc, x, out):
             square(b, ORDER[1])
             if b > 0:
                 total(b - 1, range(N_OFF))
-            if b + 1 < B:
-                quantise(b + 1, [UP])
             if b > 0:
                 root(b - 1, range(N_OFF))
             if b < B - 1:
@@ -304,7 +317,6 @@ def tile_cofeature_fast_pa_t_kernel(tc, x, out):
             if turning < B:
                 transpose_map(turning, CENTER)
                 copy_out(turning, CENTER, on_vector=False)
-                raise_rows(turning)
             if b % 2 == 0 and FIRST_LOADS + b // 2 < len(LOADS):
                 load(FIRST_LOADS + b // 2)
             if b > 0:
@@ -322,10 +334,10 @@ def tile_cofeature_fast_pa_t_kernel(tc, x, out):
             if turning < B:
                 transpose_map(turning, LEFT)
                 copy_out(turning, LEFT, on_vector=False)
+            transpose_map(b + 1, RIGHT)
+            copy_out(b + 1, RIGHT, on_vector=(b % 2 == 1))
             product(b, ORDER[3])
             square(b, ORDER[3])
-            transpose_map(b + 1, RIGHT)
-            copy_out(b + 1, RIGHT, on_vector=False)
             product(b, ORDER[4])
             square(b, ORDER[4])
             if turning < B:

from contextlib import ExitStack

import concourse.mybir as mybir
from concourse.masks import make_identity

F32 = mybir.dt.float32
BF16 = mybir.dt.bfloat16
I32 = mybir.dt.int32
U32 = mybir.dt.uint32
U8 = mybir.dt.uint8
FP8X4 = mybir.dt.float8_e4m3fn_x4
SQUARE = mybir.ActivationFunctionType.Square
COPY = mybir.ActivationFunctionType.Copy
MULT = mybir.AluOpType.mult
ADD = mybir.AluOpType.add

B, C, H, W = 16, 256, 16, 32
K = H * W
EPS = 1e-12
P = 128
HALVES = C // P
PACK = 4
BLOCK_P = 8
SHIFTED_P = P - BLOCK_P
GROUP_P = 32
GROUP_ROWS = GROUP_P // BLOCK_P

LEFT, CENTER, RIGHT = 0, 1, 2
MAPS = 3
OFFSETS = [(LEFT, True), (CENTER, True), (RIGHT, True), (LEFT, False), (CENTER, False)]
N_OFF = len(OFFSETS)
ORDER = [3, 4, 0, 1, 2]
STORES = [[0, 1], [2], [3, 4]]
KEPT = 3
AHEAD = 2
LOADS = [(0, 1), (1, 1)] + [(b, 2) for b in range(2, B, 2)]
FIRST_LOADS = 4

FLOPS = 2 * B * N_OFF * C * C * K


def tile_cofeature_fast_pa_t_kernel(tc, x, out):
    nc = tc.nc
    with ExitStack() as ctx:
        const = ctx.enter_context(tc.tile_pool(name="const", bufs=1))
        stage = ctx.enter_context(tc.tile_pool(name="stage", bufs=3 * MAPS))
        packed = ctx.enter_context(tc.tile_pool(name="packed", bufs=3))
        planes = ctx.enter_context(tc.tile_pool(name="planes", bufs=AHEAD + 3))
        small = ctx.enter_context(tc.tile_pool(name="small", bufs=3))
        results = ctx.enter_context(tc.tile_pool(name="results", bufs=3 * len(STORES)))
        psum_t = ctx.enter_context(tc.psum_pool(name="psum_t", bufs=2))
        psum_g = ctx.enter_context(tc.psum_pool(name="psum_g", bufs=6))
        ctx.enter_context(tc.manual_schedule())

        identity = const.tile([P, P], F32)
        make_identity(nc, identity[:])
        ones = const.tile([P, P], F32)
        nc.vector.memset(ones[:], 1.0)
        warm = const.tile([P, 1], F32)
        nc.scalar.sqrt(out=warm[:], in_=ones[:, 0:1])
        edges = []
        raised = []
        raised_scales = []
        for e in range(AHEAD + 1):
            edge = const.tile([P, C], U32, name="edge%d" % e, align_bytes=64)
            nc.vector.memset(edge[:].bitcast(I32), 0)
            edges.append(edge)
            up = const.tile([P, C], U32, name="up%d" % e, align_bytes=64)
            nc.vector.memset(up[:].bitcast(I32), 0)
            raised.append(up)
            up_scales = const.tile([P, C], U8, name="up_scales%d" % e, align_bytes=64)
            nc.vector.memset(up_scales[:].bitcast(I32), 0)
            raised_scales.append(up_scales)

        image = {}
        inner_of = {}
        seams_of = {}
        turned_of = {}
        grouped_of = {}
        codes_of = {}
        scales_of = {}
        partial_of = {}
        sums_of = {}
        floored_of = {}
        norm_of = {}
        inverse_of = {}
        result_of = {}
        stored_of = {}

        def load(n):
            first, count = LOADS[n]
            x_sb = const.tile([P, count, HALVES * K], BF16, name="x%d" % first)
            nc.sync.dma_start(
                out=x_sb[:], in_=x[first : first + count].rearrange("b (p h) i j -> p b (h i j)", h=HALVES)
            )
            for e in range(count):
                image[first + e] = x_sb[:, e, :]

        def copy_on_gpsimd(dst, src):
            nc.gpsimd.tensor_scalar(out=dst, in0=src, scalar1=1.0, scalar2=0.0, op0=MULT, op1=ADD)

        def copy_on_vector(dst, src):
            nc.vector.tensor_copy(out=dst, in_=src)

        def shift_inner(b):
            inner = planes.tile([P, HALVES, P, 2], BF16)
            copy_on_vector(
                inner[:].rearrange("p h m e -> p (h m) e"),
                image[b].rearrange("p (w t) -> p w t", t=PACK)[:, :, 1:3],
            )
            inner_of[b] = inner

        def shift_seams(b, copy):
            seams = planes.tile([P, (HALVES * H + 1) * W // 2], BF16)
            rows = image[b].rearrange("p (r j) -> p r j", j=W)
            words = seams[:, 0 : HALVES * P * 2].rearrange("p (r q e) -> p r q e", q=BLOCK_P, e=2)
            copy(
                words[:, :, 1:BLOCK_P, :],
                rows[:, :, PACK - 1 : W - 1].rearrange("p r (q t) -> p r q t", t=PACK)[:, :, :, 0:2],
            )
            copy(words[:, :, 0, :], rows[:, :, 0:1].to_broadcast([P, HALVES * H, 2]))
            seams_of[b] = seams

        def replace_borders(b, copy):
            words = seams_of[b][:, W // 2 :].rearrange("p (r v) -> p r v", v=W // 2)
            rows = image[b].rearrange("p (r j) -> p r j", j=W)
            copy(words[:, :, 0:2], rows[:, :, W - 1 : W].to_broadcast([P, HALVES * H, 2]))

        def transpose_map(b, m):
            turned = psum_t.tile([P, HALVES, 2, P], F32)
            for h in range(HALVES):
                for u in range(2):
                    if m == CENTER:
                        words = image[b].bitcast(F32).rearrange("p (h w u) -> p h u w", h=HALVES, u=2)[:, h, u, :]
                    elif (m == LEFT) == (u == 1):
                        words = inner_of[b][:, h].rearrange("p m e -> p (m e)").bitcast(F32)
                    else:
                        start = h * P + (1 if m == RIGHT else 0)
                        words = seams_of[b][:].bitcast(F32)[:, start : start + P]
                    nc.tensor.transpose(turned[:, h, u, :], words, identity[:])
            turned_of[(b, m)] = turned

        def copy_out(b, m, on_vector):
            grouped = stage.tile([P, C * PACK], BF16, align_bytes=64)
            copy = nc.vector.tensor_copy if on_vector else nc.scalar.copy
            copy(
                out=grouped[:].bitcast(F32).rearrange("p (h m u) -> p h m u", h=HALVES, u=2),
                in_=turned_of[(b, m)][:].rearrange("p h u m -> p h m u"),
            )
            grouped_of[(b, m)] = grouped

        def raise_rows(b):
            codes, scales = codes_of[b][:, CENTER, :], scales_of[b][:, CENTER, :]
            up, up_scales = raised[b % len(raised)], raised_scales[b % len(raised)]
            nc.sync.dma_start(out=up[0:SHIFTED_P, :].bitcast(I32), in_=codes[BLOCK_P:P, :].bitcast(I32))
            for r in range(GROUP_ROWS - 1):
                nc.sync.dma_start(
                    out=up_scales[r:P:GROUP_P, :].bitcast(I32), in_=scales[r + 1 : P : GROUP_P, :].bitcast(I32)
                )
            nc.sync.dma_start(
                out=up_scales[GROUP_ROWS - 1 : P - GROUP_P : GROUP_P, :].bitcast(I32),
                in_=scales[GROUP_P:P:GROUP_P, :].bitcast(I32),
            )

        def quantise(b, maps):
            if b not in codes_of:
                codes = packed.tile([P, MAPS, C], U32, align_bytes=64)
                scales = packed.tile([P, MAPS, C], U8, align_bytes=64)
                codes_of[b] = codes
                scales_of[b] = scales
            for m in maps:
                nc.vector.quantize_mx(
                    out=codes_of[b][:, m, :].bitcast(FP8X4), scales=scales_of[b][:, m, :], in_=grouped_of[(b, m)][:]
                )

        def copy_edge(b):
            nc.sync.dma_start(
                out=edges[b % len(edges)][0:BLOCK_P, :].bitcast(I32),
                in_=codes_of[b][0:BLOCK_P, CENTER, :].bitcast(I32),
            )

        def in_output_order(sums):
            return sums[:].rearrange("p h (g m) -> p h m g", g=HALVES)

        def product(b, o):
            codes, scales, edge = codes_of[b], scales_of[b], edges[b % len(edges)]
            up, up_scales = raised[b % len(raised)], raised_scales[b % len(raised)]
            m, row_above = OFFSETS[o]
            sums = psum_g.tile([P, HALVES, C], F32)
            for h in range(HALVES):
                cols = slice(h * P, (h + 1) * P)
                if row_above:
                    stationary = [(up[:, cols], up_scales[:, cols]), (edge[:, cols], scales[:, CENTER, cols])]
                else:
                    stationary = [(codes[:, CENTER, cols], scales[:, CENTER, cols])]
                for n, (words, plane) in enumerate(stationary):
                    nc.tensor.matmul_mx(
                        out=sums[:, h, :],
                        lhsT=words.bitcast(FP8X4),
                        lhsT_scale=plane,
                        rhs=codes[:, m, :].bitcast(FP8X4),
                        rhs_scale=scales[:, m, :],
                        start=(n == 0),
                        stop=(n == len(stationary) - 1),
                    )
            sums_of[(b, o)] = sums

        def square(b, o):
            squared = small.tile([P, HALVES * C], F32)
            nc.scalar.activation(
                out=squared[:],
                in_=sums_of[(b, o)][:].rearrange("p h d -> p (h d)"),
                func=SQUARE,
                accum_out=partial_of[b][:, o : o + 1],
            )

        def unload(b, o):
            nc.vector.tensor_copy(
                out=result_tile(b, o).rearrange("p (h m g) -> p h m g", h=HALVES, g=HALVES),
                in_=in_output_order(sums_of[(b, o)]),
            )

        def result_tile(b, o):
            if (b, o) not in result_of:
                group = [g for g in STORES if o in g][0]
                results_sb = results.tile([P, len(group), HALVES * C], F32)
                for n, member in enumerate(group):
                    result_of[(b, member)] = results_sb[:, n, :]
                stored_of[(b, group[0])] = results_sb
            return result_of[(b, o)]

        def store(b, offsets):
            for group in STORES:
                if group[0] in offsets:
                    nc.sync.dma_start(
                        out=out[b, group[0] : group[-1] + 1].rearrange("o (p f) -> p o f", p=P),
                        in_=stored_of[(b, group[0])][:],
                    )

        def total(b, offsets):
            these = slice(min(offsets), max(offsets) + 1)
            turned = psum_t.tile([P, HALVES, 2, P], F32)
            summed = turned[:, 0, 0, 0:N_OFF]
            nc.tensor.matmul(out=summed[:, these], lhsT=ones[:], rhs=partial_of[b][:, these], start=True, stop=True)
            floored = small.tile([P, N_OFF], F32)
            nc.vector.tensor_scalar_max(out=floored[:, these], in0=summed[:, these], scalar1=EPS * EPS)
            floored_of[b] = floored

        def root(b, offsets):
            these = slice(min(offsets), max(offsets) + 1)
            norm = small.tile([P, N_OFF], F32)
            nc.scalar.sqrt(out=norm[:, these], in_=floored_of[b][:, these])
            norm_of[b] = norm

        def invert(b, offsets):
            these = slice(min(offsets), max(offsets) + 1)
            inverse = small.tile([P, N_OFF], F32)
            nc.vector.reciprocal(out=inverse[:, these], in_=norm_of[b][:, these])
            inverse_of[b] = inverse

        def scale_out(b, o, halves=(0, HALVES), on_vector=True):
            these = slice(*halves)
            result = result_tile(b, o).rearrange("p (h m g) -> p h m g", h=HALVES, g=HALVES)[:, these]
            sums = in_output_order(sums_of[(b, o)])[:, these]
            factor = inverse_of[b][:, o : o + 1]
            if on_vector:
                nc.vector.tensor_scalar_mul(out=result, in0=sums, scalar1=factor)
            else:
                nc.scalar.activation(out=result, in_=sums, func=COPY, scale=factor)

        def scale_in_place(b, o):
            result = result_tile(b, o)
            factor = inverse_of[b][:, o : o + 1]
            nc.gpsimd.tensor_scalar(out=result, in0=result, scalar1=factor, scalar2=0.0, op0=MULT, op1=ADD)

        for n in range(FIRST_LOADS):
            load(n)
        for b in range(AHEAD):
            copy = copy_on_vector if b == 0 else copy_on_gpsimd
            shift_inner(b)
            shift_seams(b, copy)
            transpose_map(b, CENTER)
            copy_out(b, CENTER, on_vector=False)
            transpose_map(b, LEFT)
            copy_out(b, LEFT, on_vector=True)
            replace_borders(b, copy)
            if b == 0:
                transpose_map(b, RIGHT)
                copy_out(b, RIGHT, on_vector=False)
                quantise(b, [CENTER, LEFT, RIGHT])
                copy_edge(b)
                raise_rows(b)
        for b in (AHEAD, AHEAD + 1):
            shift_inner(b)
            shift_seams(b, copy_on_gpsimd)
        for b in range(B):
            turning = b + AHEAD
            partial = small.tile([P, N_OFF], F32)
            partial_of[b] = partial
            product(b, ORDER[0])
            square(b, ORDER[0])
            if b + 1 < B:
                quantise(b + 1, [CENTER])
                copy_edge(b + 1)
                raise_rows(b + 1)
                quantise(b + 1, [LEFT])
            if b > 0:
                quantise(b, [RIGHT])
            product(b, ORDER[1])
            square(b, ORDER[1])
            if b > 0:
                total(b - 1, range(N_OFF))
            if b > 0:
                root(b - 1, range(N_OFF))
            if b < B - 1:
                unload(b, ORDER[0])
            if turning < B:
                transpose_map(turning, CENTER)
                copy_out(turning, CENTER, on_vector=False)
            if b % 2 == 0 and FIRST_LOADS + b // 2 < len(LOADS):
                load(FIRST_LOADS + b // 2)
            if b > 0:
                invert(b - 1, range(N_OFF))
                for o in ORDER[-KEPT:]:
                    scale_out(b - 1, o)
                for o in ORDER[:-KEPT]:
                    scale_in_place(b - 1, o)
                store(b - 1, range(N_OFF))
            if b == B - 1:
                break
            unload(b, ORDER[1])
            product(b, ORDER[2])
            square(b, ORDER[2])
            if turning < B:
                transpose_map(turning, LEFT)
                copy_out(turning, LEFT, on_vector=False)
            transpose_map(b + 1, RIGHT)
            copy_out(b + 1, RIGHT, on_vector=(b % 2 == 1))
            product(b, ORDER[3])
            square(b, ORDER[3])
            product(b, ORDER[4])
            square(b, ORDER[4])
            if turning < B:
                replace_borders(turning, copy_on_gpsimd)
            if turning + 2 < B:
                shift_inner(turning + 2)
                shift_seams(turning + 2, copy_on_gpsimd)

        b = B - 1
        first, second, last = [3, 4], [0, 1], [2]
        total(b, first)
        root(b, first)
        invert(b, first)
        for o in first:
            scale_out(b, o)
        store(b, first)
        for o in second:
            product(b, o)
            square(b, o)
        product(b, last[0])
        total(b, second)
        square(b, last[0])
        root(b, second)
        invert(b, second)
        total(b, last)
        scale_out(b, second[0])
        root(b, last)
        scale_out(b, second[1], on_vector=False)
        store(b, second)
        invert(b, last)
        scale_out(b, last[0], halves=(0, 1))
        scale_out(b, last[0], halves=(1, 2), on_vector=False)
        store(b, last)
